import numpy as np
import ml_dtypes


def mxq(x, axis, fmt="e4m3"):
    dtype, down = {"e4m3": (ml_dtypes.float8_e4m3fn, 7), "e5m2": (ml_dtypes.float8_e5m2, 14)}[fmt]
    v = np.moveaxis(np.asarray(x, np.float32).astype(ml_dtypes.bfloat16).astype(np.float64), axis, -1)
    blocks = v.reshape(v.shape[:-1] + (-1, 32))
    amax = np.abs(blocks).max(-1, keepdims=True)
    byte = np.maximum(np.where(amax > 0, np.frexp(amax)[1] - 1 + 127, 0) - down, 1)
    scale = np.exp2(byte - 127.0)
    codes = (blocks / scale).astype(np.float32).astype(dtype).astype(np.float64)
    return np.moveaxis((codes * scale).reshape(v.shape), -1, axis)


WIDE = False


def mx_kscale(k):
    if not WIDE:
        return np.ones(k)
    levels = np.array([18, -18])
    if k % 512:
        return np.exp2(np.random.permutation(np.resize(levels, k // 32))).repeat(32)
    a = np.empty((k // 512, 16))
    for p in range(k // 512):
        a[p, :8] = np.random.permutation(np.resize(levels, 8))
        for g in range(8):
            far = levels[np.abs(levels - a[p, g]) >= 10]
            a[p, g + 8] = far[np.random.randint(len(far))]
    return np.exp2(a.ravel()).repeat(32)


BF16 = ml_dtypes.bfloat16


def bf(x):
    return np.asarray(x, np.float32).astype(BF16)


def f64(x):
    return np.asarray(x).astype(np.float64)


D_DIM, T_DIM, M_DIM = 1024, 1536, 1536
C_INIT = 1.0


def setup_inputs():
    s = mx_kscale(T_DIM)[None, :]
    u = mx_kscale(D_DIM)[:, None]
    Z = bf(0.2 * np.random.standard_normal((D_DIM, T_DIM)))
    x0 = bf(np.random.standard_normal((M_DIM, T_DIM)))
    U = bf(2.0 / np.sqrt(D_DIM) * np.random.standard_normal((D_DIM, D_DIM)))
    v0 = bf(0.4 / np.sqrt(M_DIM) * np.random.standard_normal((D_DIM, M_DIM)))
    l1 = bf(np.random.uniform(0.08, 0.12, 1))
    g = bf(4.0 * np.random.standard_normal((D_DIM, T_DIM)) * np.exp2(np.random.randint(-6, 1, (1, T_DIM))) / s * u)
    mat = f64(U) @ f64(Z) + f64(v0) @ f64(x0)
    return {"Z": Z,
            "X": bf(f64(x0) * s),
            "U": U,
            "V": bf(f64(v0) / u),
            "l1": l1,
            "mat": np.asarray(mat, np.float32),
            "grad_out": g}


def reference(Z, X, U, V, l1, mat, grad_out):
    thres = f64(l1) / C_INIT
    dmat = np.where(np.abs(f64(mat)) > thres, f64(grad_out), 0.0)
    dX = mxq(f64(V), 0, "e4m3").T @ mxq(dmat, 0, "e5m2")
    dV = mxq(dmat, 1, "e5m2") @ mxq(f64(X), 1, "e4m3").T
    return dX, dV

@@ -1,0 +1,353 @@
+from contextlib import ExitStack
+
+import concourse.mybir as mybir
+from concourse.masks import make_identity
+
+D, T, M = 1024, 1536, 1536
+FLOPS = 2 * 2 * D * T * M
+BYTES = 2 * (M * T + D * M + D * T) + 4 * (D * T + M * T + D * M) + 2
+
+F32 = mybir.dt.float32
+BF16 = mybir.dt.bfloat16
+U32 = mybir.dt.uint32
+U8 = mybir.dt.uint8
+I32 = mybir.dt.int32
+E4M3 = mybir.dt.float8_e4m3fn_x4
+E5M2 = mybir.dt.float8_e5m2_x4
+ALU = mybir.AluOpType
+ABS = mybir.ActivationFunctionType.Abs
+
+P = 128
+K = 512
+N = 512
+DG = D // K
+TG = T // K
+MC = M // N
+
+
+def tile_blueboxlayer_pb_v_kernel(tc, Z, X, U, V, l1, mat, grad_out, out_0, out_1):
+    nc = tc.nc
+    with ExitStack() as ctx:
+        const = ctx.enter_context(tc.tile_pool(name="const", bufs=1))
+        raw = ctx.enter_context(tc.tile_pool(name="raw", bufs=5))
+        keep = ctx.enter_context(tc.tile_pool(name="keep", bufs=1))
+        work = ctx.enter_context(tc.tile_pool(name="work", bufs=3))
+        outs = ctx.enter_context(tc.tile_pool(name="outs", bufs=7))
+        psum = ctx.enter_context(tc.psum_pool(name="psum", bufs=8))
+        ctx.enter_context(tc.manual_schedule())
+
+        thres = const.tile([P, 1], BF16, name="thres")
+        nc.scalar.dma_start(out=thres[:], in_=l1.partition_broadcast(P))
+        ident = const.tile([P, P], F32, name="ident")
+        make_identity(nc, ident[:])
+
+        mat_v = mat.rearrange("(g p j) t -> g p j t", g=DG, j=4)
+        grad_v = grad_out.rearrange("(g p j) t -> g p j t", g=DG, j=4)
+        v_v = V.rearrange("(g p j) m -> g p j m", g=DG, j=4)
+        x_v = X.rearrange("(c p i) t -> c p i t", c=MC, i=4)
+        mats, xs, vs = {}, {}, {}
+        grads = [keep.tile([P, 4, T], BF16, name="grad%d" % g, align_bytes=64) for g in range(DG)]
+        dmat = grads
+
+        def raw_tile(store, key, shape, dtype):
+            if key not in store:
+                store[key] = raw.tile(shape, dtype, name="raw_tile", tag="raw", align_bytes=64)
+            return store[key]
+
+        def load_mat(g, j, n=1):
+            t = raw_tile(mats, (g, j // 2), [P, 2, T], F32)
+            nc.sync.dma_start(out=t[:, j % 2 : j % 2 + n, :], in_=mat_v[g, :, j : j + n, :])
+
+        def load_grad(g, h, n=1):
+            nc.sync.dma_start(out=grads[g][:, 2 * h : 2 * h + 2 * n, :], in_=grad_v[g, :, 2 * h : 2 * h + 2 * n, :])
+
+        def load_x(b, n=1):
+            t = raw_tile(xs, b // 2, [P, 4, T], BF16)
+            i = 2 * (b % 2)
+            nc.sync.dma_start(out=t[:, i : i + 2 * n, :], in_=x_v[b // 2, :, i : i + 2 * n, :])
+
+        def load_v(g):
+            t = raw_tile(vs, g, [P, 4, M], BF16)
+            nc.sync.dma_start(out=t[:], in_=v_v[g])
+
+        load_mat(0, 0)
+        load_grad(0, 0)
+        load_mat(0, 1)
+        load_x(0)
+        load_x(1)
+        load_mat(0, 2)
+        load_grad(0, 1)
+        load_mat(0, 3)
+        load_x(2)
+        load_x(3)
+        load_x(4, 2)
+        load_mat(1, 0, 2)
+        load_grad(1, 0, 2)
+        load_mat(1, 2, 2)
+        load_v(0)
+        load_v(1)
+        dt_codes = [keep.tile([P, TG, K], U32, name="dt_codes%d" % g, align_bytes=64) for g in range(DG)]
+        dt_scales = [keep.tile([P, TG, K], U8, name="dt_scales%d" % g, align_bytes=64) for g in range(DG)]
+        x_codes = [keep.tile([P, TG, N], U32, name="x_codes%d" % c, align_bytes=64) for c in range(MC)]
+        x_scales = [keep.tile([P, TG, N], U8, name="x_scales%d" % c, align_bytes=64) for c in range(MC)]
+        d_codes = [keep.tile([P, DG, N], U32, name="d_codes%d" % s, align_bytes=64) for s in range(TG)]
+        d_scales = [keep.tile([P, DG, N], U8, name="d_scales%d" % s, align_bytes=64) for s in range(TG)]
+        v_codes = [keep.tile([P, DG, N], U32, name="v_codes%d" % c, align_bytes=64) for c in range(MC)]
+        v_scales = [keep.tile([P, DG, N], U8, name="v_scales%d" % c, align_bytes=64) for c in range(MC)]
+
+        def evac(engine, out, in_):
+            if engine == "S":
+                nc.scalar.copy(out=out, in_=in_)
+            else:
+                nc.vector.tensor_copy(out=out, in_=in_)
+
+        def absolute(g, j, engine):
+            row = mats[g, j // 2][:, j % 2, :]
+            if engine == "S":
+                nc.scalar.activation(out=row, in_=row, func=ABS)
+            else:
+                bits = row.bitcast(I32)
+                nc.vector.tensor_scalar(out=bits, in0=bits, scalar1=0x7FFFFFFF, scalar2=None, op0=ALU.bitwise_and)
+
+        def mask(g, j):
+            nc.vector.scalar_tensor_tensor(
+                out=dmat[g][:, j, :], in0=mats[g, j // 2][:, j % 2, :], scalar=thres[:, 0:1],
+                in1=grads[g][:, j, :], op0=ALU.is_gt, op1=ALU.mult)
+
+        dt_rows, x_rows = {}, {}
+
+        def words_of(rows):
+            return rows.rearrange("p i t -> p (i t)").bitcast(F32)
+
+        def transpose_d(g, h, engines):
+            words = words_of(dmat[g][:, 2 * h : 2 * h + 2, :])
+            for s in range(TG):
+                if h == 0:
+                    dt_rows[g, s] = work.tile([P, K * 4], BF16, name="dt_rows", tag="dt_rows", align_bytes=64)
+                bank = psum.tile([P, 4, P], F32, name="bank_t", tag="bank")
+                for i in range(2):
+                    for u in range(2):
+                        first = i * (T // 2) + 256 * s + u
+                        nc.tensor.transpose(bank[:, 2 * i + u, :], words[:, first : first + 255 : 2], ident[:])
+                evac(engines[s],
+                     dt_rows[g, s][:].bitcast(F32).rearrange("q (i p u) -> q i p u", i=4, u=2)[:, 2 * h : 2 * h + 2],
+                     bank[:].rearrange("q (i u) p -> q i p u", u=2))
+
+        def quantize_dt(g, s, h):
+            half = slice(h * K // 2, (h + 1) * K // 2)
+            nc.vector.quantize_mx(out=dt_codes[g][:, s, half].bitcast(E5M2), scales=dt_scales[g][:, s, half],
+                                  in_=dt_rows[g, s][:, h * 2 * K : (h + 1) * 2 * K])
+
+        def transpose_x(b, engines):
+            c, h = b // 2, b % 2
+            words = words_of(xs[c][:, 2 * h : 2 * h + 2, :])
+            for s in range(TG):
+                if h == 0:
+                    x_rows[c, s] = work.tile([P, N * 4], BF16, name="x_rows", tag="x_rows", bufs=5, align_bytes=64)
+                bank = psum.tile([P, 4, P], F32, name="bank_t", tag="bank")
+                for i in range(2):
+                    for u in range(2):
+                        first = i * (T // 2) + 256 * s + u
+                        nc.tensor.transpose(bank[:, 2 * i + u, :], words[:, first : first + 255 : 2], ident[:])
+                evac(engines[s],
+                     x_rows[c, s][:].bitcast(F32).rearrange("q (p h w) -> q p h w", h=2, w=4)[:, :, h],
+                     bank[:].rearrange("q w p -> q p w"))
+
+        def quantize_x(c, s):
+            nc.vector.quantize_mx(out=x_codes[c][:, s, :].bitcast(E4M3), scales=x_scales[c][:, s, :], in_=x_rows[c, s][:])
+
+        grouped = {}
+
+        def group(key, src, cols):
+            t = work.tile([P, N, 4], BF16, name="grouped", tag="grouped", bufs=2, align_bytes=64)
+            nc.vector.tensor_copy(
+                out=t[:].rearrange("p (c i) j -> p c j i", i=4),
+                in_=src[:, :, cols].rearrange("p j (c i) -> p c j i", i=4))
+            grouped[key] = t
+
+        def group_d(g, s):
+            group(("d", g, s), dmat[g], slice(s * N, s * N + N))
+
+        def quantize_d(g, s):
+            nc.vector.quantize_mx(out=d_codes[s][:, g, :].bitcast(E5M2), scales=d_scales[s][:, g, :],
+                                  in_=grouped["d", g, s][:].rearrange("p n j -> p (n j)"))
+
+        def group_v(g, c):
+            group(("v", g, c), vs[g], slice(c * N, c * N + N))
+
+        def quantize_v(g, c):
+            nc.vector.quantize_mx(out=v_codes[c][:, g, :].bitcast(E4M3), scales=v_scales[c][:, g, :],
+                                  in_=grouped["v", g, c][:].rearrange("p n j -> p (n j)"))
+
+        out_1v = out_1.rearrange("(g p j) m -> g j p m", g=DG, j=4)
+        out_0v = out_0.rearrange("(b p) t -> b p t", p=P)
+        stages = {}
+
+        def stage_tile(key, width):
+            if key not in stages:
+                stages[key] = outs.tile([P, width], F32, name="stage", tag="stage")
+            return stages[key]
+
+        done = {}
+
+        def product_1(g, j, c, engine):
+            stage = stage_tile((1, g, j), M)
+            bank = psum.tile([P, N], F32, name="bank_1", tag="bank")
+            cols = slice(j * P, j * P + P)
+            for s in range(TG):
+                nc.tensor.matmul_mx(
+                    out=bank[:], lhsT=dt_codes[g][:, s, cols].bitcast(E5M2), lhsT_scale=dt_scales[g][:, s, cols],
+                    rhs=x_codes[c][:, s, :].bitcast(E4M3), rhs_scale=x_scales[c][:, s, :],
+                    start=(s == 0), stop=(s == TG - 1))
+            evac(engine, stage[:, c * N : c * N + N], bank[:])
+            done[1, g, j] = done.get((1, g, j), 0) + 1
+            if done[1, g, j] == MC:
+                nc.sync.dma_start(out=out_1v[g, j], in_=stage[:])
+
+        def product_0(b, s, engine):
+            stage = stage_tile((0, b), T)
+            c, cols, toks = b // 4, slice((b % 4) * P, (b % 4) * P + P), slice(s * N, s * N + N)
+            bank = psum.tile([P, N], F32, name="bank_0", tag="bank")
+            for g in range(DG):
+                nc.tensor.matmul_mx(
+                    out=bank[:], lhsT=v_codes[c][:, g, cols].bitcast(E4M3), lhsT_scale=v_scales[c][:, g, cols],
+                    rhs=d_codes[s][:, g, :].bitcast(E5M2), rhs_scale=d_scales[s][:, g, :],
+                    start=(g == 0), stop=(g == DG - 1))
+            evac(engine, stage[:, toks], bank[:])
+            done[0, b] = done.get((0, b), 0) + 1
+            if b == 4 * MC - 1:
+                nc.sync.dma_start(out=out_0v[b, :, toks], in_=stage[:, toks])
+            elif done[0, b] == TG:
+                nc.sync.dma_start(out=out_0v[b], in_=stage[:])
+
+        absolute(0, 0, "S")
+        mask(0, 0)
+        absolute(0, 1, "S")
+        mask(0, 1)
+        transpose_x(0, "SVS")
+        transpose_d(0, 0, "SVV")
+        transpose_x(1, "VSS")
+        quantize_dt(0, 0, 0)
+        quantize_dt(0, 1, 0)
+        quantize_dt(0, 2, 0)
+        quantize_x(0, 0)
+        quantize_x(0, 1)
+        quantize_x(0, 2)
+        absolute(0, 2, "V")
+        absolute(0, 3, "S")
+        mask(0, 2)
+        product_1(0, 0, 0, "S")
+        mask(0, 3)
+        group_d(0, 0)
+        transpose_x(2, "VSS")
+        transpose_x(3, "SSS")
+        group_d(0, 1)
+        transpose_d(0, 1, "SSS")
+        quantize_x(1, 0)
+        quantize_x(1, 1)
+        quantize_x(1, 2)
+        transpose_x(4, "VSS")
+        quantize_dt(0, 0, 1)
+        quantize_dt(0, 1, 1)
+        quantize_dt(0, 2, 1)
+        transpose_x(5, "SSS")
+        quantize_d(0, 0)
+        absolute(1, 0, "S")
+        absolute(1, 1, "S")
+        product_1(0, 1, 0, "S")
+        product_1(0, 2, 0, "S")
+        product_1(0, 3, 0, "S")
+        quantize_x(2, 0)
+        quantize_x(2, 1)
+        quantize_x(2, 2)
+        quantize_d(0, 1)
+        product_1(0, 0, 1, "S")
+        mask(1, 0)
+        product_1(0, 1, 1, "S")
+        product_1(0, 2, 1, "S")
+        product_1(0, 3, 1, "S")
+        mask(1, 1)
+        product_1(0, 0, 2, "S")
+        transpose_d(1, 0, "SSS")
+        absolute(1, 2, "V")
+        mask(1, 2)
+        product_1(0, 1, 2, "S")
+        quantize_dt(1, 0, 0)
+        quantize_dt(1, 1, 0)
+        quantize_dt(1, 2, 0)
+        product_1(0, 2, 2, "S")
+        product_1(0, 3, 2, "S")
+        absolute(1, 3, "V")
+        product_1(1, 0, 0, "S")
+        product_1(1, 0, 1, "S")
+        product_1(1, 0, 2, "S")
+        mask(1, 3)
+        group_v(0, 0)
+        group_d(0, 2)
+        transpose_d(1, 1, "SSS")
+        product_1(1, 1, 0, "S")
+        product_1(1, 1, 1, "S")
+        product_1(1, 1, 2, "S")
+        quantize_dt(1, 0, 1)
+        quantize_dt(1, 1, 1)
+        quantize_dt(1, 2, 1)
+        quantize_v(0, 0)
+        quantize_d(0, 2)
+        group_d(1, 0)
+        group_v(1, 0)
+        quantize_d(1, 0)
+        product_1(1, 2, 0, "S")
+        product_1(1, 2, 1, "S")
+        product_1(1, 2, 2, "S")
+        group_d(1, 1)
+        quantize_v(1, 0)
+        quantize_d(1, 1)
+        product_1(1, 3, 0, "S")
+        product_1(1, 3, 1, "S")
+        product_1(1, 3, 2, "S")
+        group_d(1, 2)
+        quantize_d(1, 2)
+        product_0(0, 0, "S")
+        product_0(1, 0, "S")
+        product_0(0, 1, "S")
+        product_0(1, 1, "S")
+        product_0(0, 2, "S")
+        product_0(1, 2, "S")
+        group_v(0, 1)
+        group_v(1, 1)
+        quantize_v(0, 1)
+        product_0(2, 0, "S")
+        product_0(2, 1, "S")
+        product_0(2, 2, "S")
+        quantize_v(1, 1)
+        group_v(1, 2)
+        product_0(3, 0, "S")
+        product_0(3, 1, "S")
+        product_0(3, 2, "S")
+        group_v(0, 2)
+        quantize_v(1, 2)
+        product_0(4, 0, "S")
+        product_0(4, 1, "S")
+        product_0(4, 2, "S")
+        quantize_v(0, 2)
+        product_0(5, 0, "S")
+        product_0(5, 1, "V")
+        product_0(5, 2, "S")
+        product_0(6, 0, "S")
+        product_0(6, 1, "V")
+        product_0(6, 2, "S")
+        product_0(7, 0, "S")
+        product_0(7, 1, "V")
+        product_0(7, 2, "S")
+        product_0(8, 0, "V")
+        product_0(8, 1, "S")
+        product_0(8, 2, "V")
+        product_0(9, 0, "S")
+        product_0(9, 1, "V")
+        product_0(9, 2, "S")
+        product_0(10, 0, "V")
+        product_0(10, 1, "S")
+        product_0(10, 2, "V")
+        product_0(11, 0, "S")
+        product_0(11, 1, "V")
+        product_0(11, 2, "S")

@@ -23,71 +23,62 @@ N = 512
 DG = D // K
 TG = T // K
 MC = M // N
+ROWS = 6
+GROUPED = 3
+D_PARTS = ((0, 1), (2,))
 
 
 def tile_blueboxlayer_pb_v_kernel(tc, Z, X, U, V, l1, mat, grad_out, out_0, out_1):
     nc = tc.nc
     with ExitStack() as ctx:
         const = ctx.enter_context(tc.tile_pool(name="const", bufs=1))
-        raw = ctx.enter_context(tc.tile_pool(name="raw", bufs=5))
+        big = ctx.enter_context(tc.tile_pool(name="big", bufs=10))
         keep = ctx.enter_context(tc.tile_pool(name="keep", bufs=1))
         work = ctx.enter_context(tc.tile_pool(name="work", bufs=3))
-        outs = ctx.enter_context(tc.tile_pool(name="outs", bufs=7))
         psum = ctx.enter_context(tc.psum_pool(name="psum", bufs=8))
         ctx.enter_context(tc.manual_schedule())
 
         thres = const.tile([P, 1], BF16, name="thres")
-        nc.scalar.dma_start(out=thres[:], in_=l1.partition_broadcast(P))
         ident = const.tile([P, P], F32, name="ident")
         make_identity(nc, ident[:])
 
         mat_v = mat.rearrange("(g p j) t -> g p j t", g=DG, j=4)
         grad_v = grad_out.rearrange("(g p j) t -> g p j t", g=DG, j=4)
         v_v = V.rearrange("(g p j) m -> g p j m", g=DG, j=4)
-        x_v = X.rearrange("(c p i) t -> c p i t", c=MC, i=4)
-        mats, xs, vs = {}, {}, {}
+        x_v = X.rearrange("(k p i) t -> k p i t", p=P, i=2)
+        out_1v = out_1.rearrange("(g p j) m -> g p j m", g=DG, j=4)
+        out_0v = out_0.rearrange("(b p) t -> p b t", p=P)
         grads = [keep.tile([P, 4, T], BF16, name="grad%d" % g, align_bytes=64) for g in range(DG)]
         dmat = grads
+        held = {}
 
-        def raw_tile(store, key, shape, dtype):
-            if key not in store:
-                store[key] = raw.tile(shape, dtype, name="raw_tile", tag="raw", align_bytes=64)
-            return store[key]
+        def big_tile(key, shape, dtype):
+            if key not in held:
+                held[key] = big.tile(shape, dtype, name="%s%d" % key, tag="big", align_bytes=64)
+            return held[key]
 
-        def load_mat(g, j, n=1):
-            t = raw_tile(mats, (g, j // 2), [P, 2, T], F32)
-            nc.sync.dma_start(out=t[:, j % 2 : j % 2 + n, :], in_=mat_v[g, :, j : j + n, :])
+        def load_thres():
+            nc.sync.dma_start(out=thres[:], in_=l1.partition_broadcast(P))
 
-        def load_grad(g, h, n=1):
-            nc.sync.dma_start(out=grads[g][:, 2 * h : 2 * h + 2 * n, :], in_=grad_v[g, :, 2 * h : 2 * h + 2 * n, :])
+        def load_mat(r, n=1):
+            g, j = divmod(r, 4)
+            t = big_tile(("mat", r // 2), [P, 2, T], F32)
+            nc.sync.dma_start(out=t[:, r % 2 : r % 2 + n, :], in_=mat_v[g, :, j : j + n, :])
 
-        def load_x(b, n=1):
-            t = raw_tile(xs, b // 2, [P, 4, T], BF16)
-            i = 2 * (b % 2)
-            nc.sync.dma_start(out=t[:, i : i + 2 * n, :], in_=x_v[b // 2, :, i : i + 2 * n, :])
+        def load_grad(r, n):
+            g, j = divmod(r, 4)
+            nc.sync.dma_start(out=grads[g][:, j : j + n, :], in_=grad_v[g, :, j : j + n, :])
+
+        def load_x(k):
+            t = big_tile(("x", k // 2), [P, 2, 2, T], BF16)
+            nc.sync.dma_start(out=t[:, k % 2], in_=x_v[k])
 
         def load_v(g):
-            t = raw_tile(vs, g, [P, 4, M], BF16)
+            t = big_tile(("v", g), [P, 4, M], BF16)
             nc.sync.dma_start(out=t[:], in_=v_v[g])
 
-        load_mat(0, 0)
-        load_grad(0, 0)
-        load_mat(0, 1)
-        load_x(0)
-        load_x(1)
-        load_mat(0, 2)
-        load_grad(0, 1)
-        load_mat(0, 3)
-        load_x(2)
-        load_x(3)
-        load_x(4, 2)
-        load_mat(1, 0, 2)
-        load_grad(1, 0, 2)
-        load_mat(1, 2, 2)
-        load_v(0)
-        load_v(1)
-        dt_codes = [keep.tile([P, TG, K], U32, name="dt_codes%d" % g, align_bytes=64) for g in range(DG)]
-        dt_scales = [keep.tile([P, TG, K], U8, name="dt_scales%d" % g, align_bytes=64) for g in range(DG)]
+        dt_codes = [keep.tile([P, TG * P], U32, name="dt_codes%d" % r, align_bytes=64) for r in range(4 * DG)]
+        dt_scales = [keep.tile([P, TG * P], U8, name="dt_scales%d" % r, align_bytes=64) for r in range(4 * DG)]
         x_codes = [keep.tile([P, TG, N], U32, name="x_codes%d" % c, align_bytes=64) for c in range(MC)]
         x_scales = [keep.tile([P, TG, N], U8, name="x_scales%d" % c, align_bytes=64) for c in range(MC)]
         d_codes = [keep.tile([P, DG, N], U32, name="d_codes%d" % s, align_bytes=64) for s in range(TG)]
@@ -101,253 +92,266 @@ def tile_blueboxlayer_pb_v_kernel(tc, Z, X, U, V, l1, mat, grad_out, out_0, out_
             else:
                 nc.vector.tensor_copy(out=out, in_=in_)
 
-        def absolute(g, j, engine):
-            row = mats[g, j // 2][:, j % 2, :]
+        def absolute(r, engine):
+            row = held["mat", r // 2][:, r % 2, :]
             if engine == "S":
                 nc.scalar.activation(out=row, in_=row, func=ABS)
             else:
                 bits = row.bitcast(I32)
                 nc.vector.tensor_scalar(out=bits, in0=bits, scalar1=0x7FFFFFFF, scalar2=None, op0=ALU.bitwise_and)
 
-        def mask(g, j):
+        def mask(r):
+            g, j = divmod(r, 4)
             nc.vector.scalar_tensor_tensor(
-                out=dmat[g][:, j, :], in0=mats[g, j // 2][:, j % 2, :], scalar=thres[:, 0:1],
+                out=dmat[g][:, j, :], in0=held["mat", r // 2][:, r % 2, :], scalar=thres[:, 0:1],
                 in1=grads[g][:, j, :], op0=ALU.is_gt, op1=ALU.mult)
 
-        dt_rows, x_rows = {}, {}
+        banks, rows = {}, {}
 
-        def words_of(rows):
-            return rows.rearrange("p i t -> p (i t)").bitcast(F32)
+        def transpose_x(k, s):
+            words = held["x", k // 2][:, k % 2].rearrange("p i t -> p (i t)").bitcast(F32)
+            bank = psum.tile([P, 4, P], F32, name="bank_x%d" % k, tag="bank")
+            for i in range(2):
+                for u in range(2):
+                    first = i * (T // 2) + 256 * s + u
+                    nc.tensor.transpose(bank[:, 2 * i + u, :], words[:, first : first + 255 : 2], ident[:])
+            banks[("x", k), s] = bank
 
-        def transpose_d(g, h, engines):
-            words = words_of(dmat[g][:, 2 * h : 2 * h + 2, :])
-            for s in range(TG):
-                if h == 0:
-                    dt_rows[g, s] = work.tile([P, K * 4], BF16, name="dt_rows", tag="dt_rows", align_bytes=64)
-                bank = psum.tile([P, 4, P], F32, name="bank_t", tag="bank")
-                for i in range(2):
-                    for u in range(2):
-                        first = i * (T // 2) + 256 * s + u
-                        nc.tensor.transpose(bank[:, 2 * i + u, :], words[:, first : first + 255 : 2], ident[:])
-                evac(engines[s],
-                     dt_rows[g, s][:].bitcast(F32).rearrange("q (i p u) -> q i p u", i=4, u=2)[:, 2 * h : 2 * h + 2],
-                     bank[:].rearrange("q (i u) p -> q i p u", u=2))
+        def transpose_d(r, part):
+            g, j = divmod(r, 4)
+            words = dmat[g][:, j, :].bitcast(F32)
+            passes = D_PARTS[part]
+            bank = psum.tile([P, len(passes), 2, P], F32, name="bank_d%d" % r, tag="bank")
+            for n, s in enumerate(passes):
+                for u in range(2):
+                    first = 256 * s + u
+                    nc.tensor.transpose(bank[:, n, u, :], words[:, first : first + 255 : 2], ident[:])
+            banks[("d", r), part] = bank
 
-        def quantize_dt(g, s, h):
-            half = slice(h * K // 2, (h + 1) * K // 2)
-            nc.vector.quantize_mx(out=dt_codes[g][:, s, half].bitcast(E5M2), scales=dt_scales[g][:, s, half],
-                                  in_=dt_rows[g, s][:, h * 2 * K : (h + 1) * 2 * K])
+        def copy_x(k, s, engine):
+            t = work.tile([P, 2 * K], BF16, name="x%d_%d" % (k, s), tag="rows", bufs=ROWS, align_bytes=64)
+            evac(engine, t[:].bitcast(F32).rearrange("q (p w) -> q p w", w=4), banks[("x", k), s][:].rearrange("q w p -> q p w"))
+            rows["x", k, s] = t
 
-        def transpose_x(b, engines):
-            c, h = b // 2, b % 2
-            words = words_of(xs[c][:, 2 * h : 2 * h + 2, :])
-            for s in range(TG):
-                if h == 0:
-                    x_rows[c, s] = work.tile([P, N * 4], BF16, name="x_rows", tag="x_rows", bufs=5, align_bytes=64)
-                bank = psum.tile([P, 4, P], F32, name="bank_t", tag="bank")
-                for i in range(2):
-                    for u in range(2):
-                        first = i * (T // 2) + 256 * s + u
-                        nc.tensor.transpose(bank[:, 2 * i + u, :], words[:, first : first + 255 : 2], ident[:])
-                evac(engines[s],
-                     x_rows[c, s][:].bitcast(F32).rearrange("q (p h w) -> q p h w", h=2, w=4)[:, :, h],
-                     bank[:].rearrange("q w p -> q p w"))
+        def copy_d(r, part, engine):
+            n = len(D_PARTS[part])
+            t = work.tile([P, n * K], BF16, name="dt%d_%d" % (r, part), tag="rows", bufs=ROWS, align_bytes=64)
+            evac(engine, t[:].bitcast(F32).rearrange("q (s p u) -> q s p u", s=n, u=2),
+                 banks[("d", r), part][:].rearrange("q s u p -> q s p u"))
+            rows["d", r, part] = t
 
-        def quantize_x(c, s):
-            nc.vector.quantize_mx(out=x_codes[c][:, s, :].bitcast(E4M3), scales=x_scales[c][:, s, :], in_=x_rows[c, s][:])
+        def quantize_x(k, s):
+            half = slice((k % 2) * N // 2, (k % 2 + 1) * N // 2)
+            nc.vector.quantize_mx(out=x_codes[k // 2][:, s, half].bitcast(E4M3), scales=x_scales[k // 2][:, s, half],
+                                  in_=rows["x", k, s][:])
+
+        def quantize_dt(r, part):
+            cols = slice(D_PARTS[part][0] * P, (D_PARTS[part][-1] + 1) * P)
+            nc.vector.quantize_mx(out=dt_codes[r][:, cols].bitcast(E5M2), scales=dt_scales[r][:, cols], in_=rows["d", r, part][:])
 
         grouped = {}
 
-        def group(key, src, cols):
-            t = work.tile([P, N, 4], BF16, name="grouped", tag="grouped", bufs=2, align_bytes=64)
-            nc.vector.tensor_copy(
-                out=t[:].rearrange("p (c i) j -> p c j i", i=4),
-                in_=src[:, :, cols].rearrange("p j (c i) -> p c j i", i=4))
+        def group(key, src, cols, engine):
+            t = work.tile([P, N, 4], BF16, name="%s%d_%d" % key, tag="grouped", bufs=GROUPED, align_bytes=64)
+            evac(engine, t[:].rearrange("p (c i) j -> p c j i", i=4), src[:, :, cols].rearrange("p j (c i) -> p c j i", i=4))
             grouped[key] = t
 
-        def group_d(g, s):
-            group(("d", g, s), dmat[g], slice(s * N, s * N + N))
+        def group_d(g, s, engine="V"):
+            group(("d", g, s), dmat[g], slice(s * N, s * N + N), engine)
 
         def quantize_d(g, s):
             nc.vector.quantize_mx(out=d_codes[s][:, g, :].bitcast(E5M2), scales=d_scales[s][:, g, :],
                                   in_=grouped["d", g, s][:].rearrange("p n j -> p (n j)"))
 
-        def group_v(g, c):
-            group(("v", g, c), vs[g], slice(c * N, c * N + N))
+        def group_v(g, c, engine="V"):
+            group(("v", g, c), held["v", g], slice(c * N, c * N + N), engine)
 
         def quantize_v(g, c):
             nc.vector.quantize_mx(out=v_codes[c][:, g, :].bitcast(E4M3), scales=v_scales[c][:, g, :],
                                   in_=grouped["v", g, c][:].rearrange("p n j -> p (n j)"))
 
-        out_1v = out_1.rearrange("(g p j) m -> g j p m", g=DG, j=4)
-        out_0v = out_0.rearrange("(b p) t -> b p t", p=P)
-        stages = {}
-
-        def stage_tile(key, width):
-            if key not in stages:
-                stages[key] = outs.tile([P, width], F32, name="stage", tag="stage")
-            return stages[key]
-
-        done = {}
-
-        def product_1(g, j, c, engine):
-            stage = stage_tile((1, g, j), M)
-            bank = psum.tile([P, N], F32, name="bank_1", tag="bank")
-            cols = slice(j * P, j * P + P)
+        def product_1(r, c):
+            bank = psum.tile([P, N], F32, name="bank_r%d" % r, tag="bank")
             for s in range(TG):
+                cols = slice(s * P, s * P + P)
                 nc.tensor.matmul_mx(
-                    out=bank[:], lhsT=dt_codes[g][:, s, cols].bitcast(E5M2), lhsT_scale=dt_scales[g][:, s, cols],
+                    out=bank[:], lhsT=dt_codes[r][:, cols].bitcast(E5M2), lhsT_scale=dt_scales[r][:, cols],
                     rhs=x_codes[c][:, s, :].bitcast(E4M3), rhs_scale=x_scales[c][:, s, :],
                     start=(s == 0), stop=(s == TG - 1))
-            evac(engine, stage[:, c * N : c * N + N], bank[:])
-            done[1, g, j] = done.get((1, g, j), 0) + 1
-            if done[1, g, j] == MC:
-                nc.sync.dma_start(out=out_1v[g, j], in_=stage[:])
+            banks["out_1", r, c] = bank
+
+        def copy_1(r, c, engine):
+            stage = big_tile(("out_1", r // 2), [P, 2, M], F32)
+            evac(engine, stage[:, r % 2, c * N : c * N + N], banks["out_1", r, c][:])
+
+        def store_1(r, n=1):
+            g, j = divmod(r, 4)
+            nc.sync.dma_start(out=out_1v[g, :, j : j + n, :], in_=held["out_1", r // 2][:, r % 2 : r % 2 + n, :])
 
         def product_0(b, s, engine):
-            stage = stage_tile((0, b), T)
-            c, cols, toks = b // 4, slice((b % 4) * P, (b % 4) * P + P), slice(s * N, s * N + N)
-            bank = psum.tile([P, N], F32, name="bank_0", tag="bank")
+            stage = big_tile(("out_0", b // 2), [P, 2, T], F32)
+            c, cols = b // 4, slice((b % 4) * P, (b % 4) * P + P)
+            bank = psum.tile([P, N], F32, name="bank_b%d" % b, tag="bank")
             for g in range(DG):
                 nc.tensor.matmul_mx(
                     out=bank[:], lhsT=v_codes[c][:, g, cols].bitcast(E4M3), lhsT_scale=v_scales[c][:, g, cols],
                     rhs=d_codes[s][:, g, :].bitcast(E5M2), rhs_scale=d_scales[s][:, g, :],
                     start=(g == 0), stop=(g == DG - 1))
-            evac(engine, stage[:, toks], bank[:])
-            done[0, b] = done.get((0, b), 0) + 1
-            if b == 4 * MC - 1:
-                nc.sync.dma_start(out=out_0v[b, :, toks], in_=stage[:, toks])
-            elif done[0, b] == TG:
-                nc.sync.dma_start(out=out_0v[b], in_=stage[:])
+            evac(engine, stage[:, b % 2, s * N : s * N + N], bank[:])
 
-        absolute(0, 0, "S")
-        mask(0, 0)
-        absolute(0, 1, "S")
-        mask(0, 1)
-        transpose_x(0, "SVS")
-        transpose_d(0, 0, "SVV")
-        transpose_x(1, "VSS")
-        quantize_dt(0, 0, 0)
-        quantize_dt(0, 1, 0)
-        quantize_dt(0, 2, 0)
-        quantize_x(0, 0)
-        quantize_x(0, 1)
-        quantize_x(0, 2)
-        absolute(0, 2, "V")
-        absolute(0, 3, "S")
-        mask(0, 2)
-        product_1(0, 0, 0, "S")
-        mask(0, 3)
+        def store_0(b, n=1, toks=slice(0, T)):
+            nc.sync.dma_start(out=out_0v[:, b : b + n, toks], in_=held["out_0", b // 2][:, b % 2 : b % 2 + n, toks])
+
+
+        load_x(0)
+        load_mat(0)
+        load_thres()
+        load_grad(0, 2)
+        load_mat(1)
+        load_x(1)
+        load_mat(2)
+        load_grad(2, 2)
+        load_x(2)
+        load_mat(3)
+        load_x(3)
+        load_x(4)
+        load_x(5)
+        for r in range(4, 8, 2):
+            load_mat(r)
+            load_grad(r, 2)
+            load_mat(r + 1)
+        load_v(0)
+        load_v(1)
+
+        def tx(k):
+            for s in range(TG):
+                transpose_x(k, s)
+
+        def cx(k, engines):
+            for s in range(TG):
+                copy_x(k, s, engines[s])
+
+        def qx(k):
+            for s in range(TG):
+                quantize_x(k, s)
+
+        def td(r):
+            for part in range(2):
+                transpose_d(r, part)
+
+        def cd(r, engines="SS"):
+            for part in range(2):
+                copy_d(r, part, engines[part])
+
+        def qd(r):
+            for part in range(2):
+                quantize_dt(r, part)
+
+        def p1(r, c, engine="S"):
+            product_1(r, c)
+            copy_1(r, c, engine)
+
+        tx(0)
+        cx(0, "VSV")
+        qx(0)
+        absolute(0, "S")
+        mask(0)
+        absolute(1, "S")
+        td(0)
+        cd(0, "SS")
+        tx(1)
+        mask(1)
+        qd(0)
+        cx(1, "SSS")
+        td(1)
+        qx(1)
+        absolute(2, "S")
+        cd(1, "SS")
+        mask(2)
+        qd(1)
+        product_1(0, 0)
+        tx(2)
+        copy_1(0, 0, "S")
+        cx(2, "SVV")
+        td(2)
+        absolute(3, "S")
+        qx(2)
+        cd(2, "SS")
+        tx(3)
+        mask(3)
+        qd(2)
+        cx(3, "SSS")
+        tx(4)
+        qx(3)
+        cx(4, "SSS")
         group_d(0, 0)
-        transpose_x(2, "VSS")
-        transpose_x(3, "SSS")
-        group_d(0, 1)
-        transpose_d(0, 1, "SSS")
-        quantize_x(1, 0)
-        quantize_x(1, 1)
-        quantize_x(1, 2)
-        transpose_x(4, "VSS")
-        quantize_dt(0, 0, 1)
-        quantize_dt(0, 1, 1)
-        quantize_dt(0, 2, 1)
-        transpose_x(5, "SSS")
+        td(3)
+        tx(5)
+        qx(4)
+        cd(3, "SS")
+        absolute(4, "S")
+        cx(5, "VVV")
+        qd(3)
+        qx(5)
+
+        p1(1, 0)
+        p1(0, 1)
+        mask(4)
         quantize_d(0, 0)
-        absolute(1, 0, "S")
-        absolute(1, 1, "S")
-        product_1(0, 1, 0, "S")
-        product_1(0, 2, 0, "S")
-        product_1(0, 3, 0, "S")
-        quantize_x(2, 0)
-        quantize_x(2, 1)
-        quantize_x(2, 2)
+        absolute(5, "S")
+        p1(1, 1)
+        p1(0, 2)
+        store_1(0)
+        group_d(0, 1)
+        absolute(6, "S")
+        mask(5)
+        p1(1, 2)
+        store_1(1)
+        td(4)
+        cd(4)
         quantize_d(0, 1)
-        product_1(0, 0, 1, "S")
-        mask(1, 0)
-        product_1(0, 1, 1, "S")
-        product_1(0, 2, 1, "S")
-        product_1(0, 3, 1, "S")
-        mask(1, 1)
-        product_1(0, 0, 2, "S")
-        transpose_d(1, 0, "SSS")
-        absolute(1, 2, "V")
-        mask(1, 2)
-        product_1(0, 1, 2, "S")
-        quantize_dt(1, 0, 0)
-        quantize_dt(1, 1, 0)
-        quantize_dt(1, 2, 0)
-        product_1(0, 2, 2, "S")
-        product_1(0, 3, 2, "S")
-        absolute(1, 3, "V")
-        product_1(1, 0, 0, "S")
-        product_1(1, 0, 1, "S")
-        product_1(1, 0, 2, "S")
-        mask(1, 3)
-        group_v(0, 0)
+        mask(6)
+        qd(4)
+        p1(2, 0)
+        absolute(7, "S")
+        p1(2, 1)
+        p1(2, 2)
+        store_1(2)
         group_d(0, 2)
-        transpose_d(1, 1, "SSS")
-        product_1(1, 1, 0, "S")
-        product_1(1, 1, 1, "S")
-        product_1(1, 1, 2, "S")
-        quantize_dt(1, 0, 1)
-        quantize_dt(1, 1, 1)
-        quantize_dt(1, 2, 1)
-        quantize_v(0, 0)
+        td(5)
+        cd(5)
+        mask(7)
         quantize_d(0, 2)
-        group_d(1, 0)
-        group_v(1, 0)
-        quantize_d(1, 0)
-        product_1(1, 2, 0, "S")
-        product_1(1, 2, 1, "S")
-        product_1(1, 2, 2, "S")
-        group_d(1, 1)
-        quantize_v(1, 0)
-        quantize_d(1, 1)
-        product_1(1, 3, 0, "S")
-        product_1(1, 3, 1, "S")
-        product_1(1, 3, 2, "S")
-        group_d(1, 2)
+        qd(5)
+        p1(3, 0)
+        p1(3, 1)
+        p1(3, 2)
+        store_1(3)
+        rest = {4: [(group_d, quantize_d, 1, 0), (group_v, quantize_v, 0, 0)], 5: [(group_v, quantize_v, 1, 0), (group_d, quantize_d, 1, 1)], 6: [(group_d, quantize_d, 1, 2)], 7: []}
+        late = []
+        for r in range(4, 8):
+            if r + 2 < 8:
+                td(r + 2)
+                cd(r + 2)
+            for n, (f, q, i, j) in enumerate(rest[r]):
+                f(i, j)
+                for args in late:
+                    args[0](*args[1:])
+                late = [(q, i, j)]
+                if n == 0 and r + 2 < 8:
+                    qd(r + 2)
+            p1(r, 0)
+            p1(r, 1)
+            p1(r, 2)
+            store_1(r)
         quantize_d(1, 2)
-        product_0(0, 0, "S")
-        product_0(1, 0, "S")
-        product_0(0, 1, "S")
-        product_0(1, 1, "S")
-        product_0(0, 2, "S")
-        product_0(1, 2, "S")
-        group_v(0, 1)
-        group_v(1, 1)
-        quantize_v(0, 1)
-        product_0(2, 0, "S")
-        product_0(2, 1, "S")
-        product_0(2, 2, "S")
-        quantize_v(1, 1)
-        group_v(1, 2)
-        product_0(3, 0, "S")
-        product_0(3, 1, "S")
-        product_0(3, 2, "S")
-        group_v(0, 2)
-        quantize_v(1, 2)
-        product_0(4, 0, "S")
-        product_0(4, 1, "S")
-        product_0(4, 2, "S")
-        quantize_v(0, 2)
-        product_0(5, 0, "S")
-        product_0(5, 1, "V")
-        product_0(5, 2, "S")
-        product_0(6, 0, "S")
-        product_0(6, 1, "V")
-        product_0(6, 2, "S")
-        product_0(7, 0, "S")
-        product_0(7, 1, "V")
-        product_0(7, 2, "S")
-        product_0(8, 0, "V")
-        product_0(8, 1, "S")
-        product_0(8, 2, "V")
-        product_0(9, 0, "S")
-        product_0(9, 1, "V")
-        product_0(9, 2, "S")
-        product_0(10, 0, "V")
-        product_0(10, 1, "S")
-        product_0(10, 2, "V")
-        product_0(11, 0, "S")
-        product_0(11, 1, "V")
-        product_0(11, 2, "S")
+
+        for b in range(12):
+            c, n = divmod(b, 4)
+            if n < 2 and c < 2:
+                group_v(n, c + 1)
+            if 0 < n < 3 and c < 2:
+                quantize_v(n - 1, c + 1)
+            for s in range(TG):
+                product_0(b, s, "S" if (n < 2 and c < 2) or (b + s) % 2 == 0 else "V")
+            store_0(b)

@@ -38,7 +38,9 @@ def tile_blueboxlayer_pb_v_kernel(tc, Z, X, U, V, l1, mat, grad_out, out_0, out_
         psum = ctx.enter_context(tc.psum_pool(name="psum", bufs=8))
         ctx.enter_context(tc.manual_schedule())
 
-        thres = const.tile([P, 1], BF16, name="thres")
+        thres = const.tile([P, 1], F32, name="thres")
+        raw = const.tile([1, 1], BF16, name="l1_raw")
+        column = const.tile([P, 1], F32, name="l1_column")
         ident = const.tile([P, P], F32, name="ident")
         make_identity(nc, ident[:])
 
@@ -58,7 +60,14 @@ def tile_blueboxlayer_pb_v_kernel(tc, Z, X, U, V, l1, mat, grad_out, out_0, out_
             return held[key]
 
         def load_thres():
-            nc.sync.dma_start(out=thres[:], in_=l1.partition_broadcast(P))
+            nc.scalar.dma_start(out=raw[:], in_=l1.rearrange("(a b) -> a b", a=1))
+            nc.vector.memset(column[:], 0.0)
+
+        def spread_thres():
+            nc.vector.tensor_copy(out=column[0:1, :], in_=raw[:])
+            bank = psum.tile([P, P], F32, name="bank_l1", tag="bank")
+            nc.tensor.transpose(bank[:], column[:].to_broadcast([P, P]), ident[:])
+            nc.vector.tensor_copy(out=thres[:], in_=bank[:, 0:1])
 
         def load_mat(r, n=1):
             g, j = divmod(r, 4)
@@ -203,9 +212,9 @@ def tile_blueboxlayer_pb_v_kernel(tc, Z, X, U, V, l1, mat, grad_out, out_0, out_
             nc.sync.dma_start(out=out_0v[:, b : b + n, toks], in_=held["out_0", b // 2][:, b % 2 : b % 2 + n, toks])
 
 
+        load_thres()
         load_x(0)
         load_mat(0)
-        load_thres()
         load_grad(0, 2)
         load_mat(1)
         load_x(1)
@@ -252,6 +261,7 @@ def tile_blueboxlayer_pb_v_kernel(tc, Z, X, U, V, l1, mat, grad_out, out_0, out_
             copy_1(r, c, engine)
 
         tx(0)
+        spread_thres()
         cx(0, "VSV")
         qx(0)
         absolute(0, "S")

@@ -50,13 +50,13 @@ def tile_blueboxlayer_pb_v_kernel(tc, Z, X, U, V, l1, mat, grad_out, out_0, out_
         x_v = X.rearrange("(k p i) t -> k p i t", p=P, i=2)
         out_1v = out_1.rearrange("(g p j) m -> g p j m", g=DG, j=4)
         out_0v = out_0.rearrange("(b p) t -> p b t", p=P)
-        grads = [keep.tile([P, 4, T], BF16, name="grad%d" % g, align_bytes=64) for g in range(DG)]
+        grads = [keep.tile([P, 4, T], BF16, name="grad%d" % g, align_bytes=256) for g in range(DG)]
         dmat = grads
         held = {}
 
         def big_tile(key, shape, dtype):
             if key not in held:
-                held[key] = big.tile(shape, dtype, name="%s%d" % key, tag="big", align_bytes=64)
+                held[key] = big.tile(shape, dtype, name="%s%d" % key, tag="big", align_bytes=256)
             return held[key]
 
         def load_thres():

@@ -213,18 +213,16 @@ def tile_blueboxlayer_pb_v_kernel(tc, Z, X, U, V, l1, mat, grad_out, out_0, out_
 
 
         load_thres()
-        load_x(0)
         load_mat(0)
         load_grad(0, 2)
+        load_x(0)
         load_mat(1)
         load_x(1)
         load_mat(2)
         load_grad(2, 2)
-        load_x(2)
         load_mat(3)
-        load_x(3)
-        load_x(4)
-        load_x(5)
+        for k in range(2, 6):
+            load_x(k)
         for r in range(4, 8, 2):
             load_mat(r)
             load_grad(r, 2)
@@ -260,14 +258,14 @@ def tile_blueboxlayer_pb_v_kernel(tc, Z, X, U, V, l1, mat, grad_out, out_0, out_
             product_1(r, c)
             copy_1(r, c, engine)
 
-        tx(0)
         spread_thres()
-        cx(0, "VSV")
-        qx(0)
         absolute(0, "S")
         mask(0)
-        absolute(1, "S")
+        tx(0)
+        cx(0, "SVV")
         td(0)
+        absolute(1, "S")
+        qx(0)
         cd(0, "SS")
         tx(1)
         mask(1)
@@ -276,75 +274,76 @@ def tile_blueboxlayer_pb_v_kernel(tc, Z, X, U, V, l1, mat, grad_out, out_0, out_
         td(1)
         qx(1)
         absolute(2, "S")
-        cd(1, "SS")
-        mask(2)
+        cd(1, "VV")
         qd(1)
+        mask(2)
         product_1(0, 0)
-        tx(2)
-        copy_1(0, 0, "S")
-        cx(2, "SVV")
-        td(2)
+        product_1(1, 0)
         absolute(3, "S")
-        qx(2)
-        cd(2, "SS")
-        tx(3)
+        copy_1(0, 0, "S")
+        copy_1(1, 0, "S")
         mask(3)
+        td(2)
+        tx(2)
+        cd(2, "SS")
+        cx(2, "SSS")
+        group_d(0, 0)
         qd(2)
+        tx(3)
         cx(3, "SSS")
+        qx(2)
+        quantize_d(0, 0)
+        td(3)
         tx(4)
         qx(3)
-        cx(4, "SSS")
-        group_d(0, 0)
-        td(3)
-        tx(5)
-        qx(4)
         cd(3, "SS")
+        cx(4, "SSS")
+        group_d(0, 1)
+        tx(5)
+        qd(3)
+        qx(4)
         absolute(4, "S")
         cx(5, "VVV")
-        qd(3)
         qx(5)
+        quantize_d(0, 1)
 
-        p1(1, 0)
         p1(0, 1)
-        mask(4)
-        quantize_d(0, 0)
-        absolute(5, "S")
         p1(1, 1)
-        p1(0, 2)
-        store_1(0)
-        group_d(0, 1)
+        mask(4)
+        absolute(5, "S")
+        p1(2, 0)
+        p1(2, 1)
+        group_d(0, 2)
         absolute(6, "S")
         mask(5)
-        p1(1, 2)
-        store_1(1)
-        td(4)
-        cd(4)
-        quantize_d(0, 1)
-        mask(6)
-        qd(4)
-        p1(2, 0)
-        absolute(7, "S")
-        p1(2, 1)
-        p1(2, 2)
-        store_1(2)
-        group_d(0, 2)
-        td(5)
-        cd(5)
-        mask(7)
-        quantize_d(0, 2)
-        qd(5)
         p1(3, 0)
         p1(3, 1)
+        quantize_d(0, 2)
+        mask(6)
+        p1(0, 2)
+        store_1(0)
+        td(4)
+        absolute(7, "S")
+        cd(4)
+        qd(4)
+        p1(1, 2)
+        store_1(1)
+        mask(7)
+        p1(2, 2)
+        store_1(2)
+        td(5)
+        cd(5)
+        qd(5)
         p1(3, 2)
         store_1(3)
-        rest = {4: [(group_d, quantize_d, 1, 0), (group_v, quantize_v, 0, 0)], 5: [(group_v, quantize_v, 1, 0), (group_d, quantize_d, 1, 1)], 6: [(group_d, quantize_d, 1, 2)], 7: []}
+        rest = {4: [(group_v, quantize_v, 0, 0), (group_d, quantize_d, 1, 0)], 5: [(group_v, quantize_v, 1, 0), (group_d, quantize_d, 1, 1)], 6: [(group_d, quantize_d, 1, 2)], 7: []}
         late = []
         for r in range(4, 8):
             if r + 2 < 8:
                 td(r + 2)
                 cd(r + 2)
             for n, (f, q, i, j) in enumerate(rest[r]):
-                f(i, j)
+                f(i, j, "S" if (f, i, j) == (group_v, 1, 0) else "V")
                 for args in late:
                     args[0](*args[1:])
                 late = [(q, i, j)]

@@ -165,6 +165,13 @@ def tile_blueboxlayer_pb_v_kernel(tc, Z, X, U, V, l1, mat, grad_out, out_0, out_
             evac(engine, t[:].rearrange("p (c i) j -> p c j i", i=4), src[:, :, cols].rearrange("p j (c i) -> p c j i", i=4))
             grouped[key] = t
 
+        def group_half(key, src, cols, half, engine):
+            if key not in grouped:
+                grouped[key] = work.tile([P, N, 4], BF16, name="%s%d_%d" % key, tag="grouped", bufs=GROUPED, align_bytes=64)
+            part = slice(half * N // 2, (half + 1) * N // 2)
+            evac(engine, grouped[key][:, part].rearrange("p (c i) j -> p c j i", i=4),
+                 src[:, :, cols][:, :, part].rearrange("p j (c i) -> p c j i", i=4))
+
         def group_d(g, s, engine="V"):
             group(("d", g, s), dmat[g], slice(s * N, s * N + N), engine)
 
@@ -298,60 +305,68 @@ def tile_blueboxlayer_pb_v_kernel(tc, Z, X, U, V, l1, mat, grad_out, out_0, out_
         qx(3)
         cd(3, "SS")
         cx(4, "SSS")
-        group_d(0, 1)
         tx(5)
         qd(3)
         qx(4)
         absolute(4, "S")
         cx(5, "VVV")
         qx(5)
-        quantize_d(0, 1)
 
-        p1(0, 1)
-        p1(1, 1)
         mask(4)
+        p1(0, 1)
         absolute(5, "S")
-        p1(2, 0)
-        p1(2, 1)
-        group_d(0, 2)
-        absolute(6, "S")
         mask(5)
+        p1(1, 1)
+        p1(2, 0)
+        absolute(6, "S")
+        group_d(0, 1)
+        p1(2, 1)
         p1(3, 0)
-        p1(3, 1)
-        quantize_d(0, 2)
         mask(6)
+        p1(3, 1)
         p1(0, 2)
         store_1(0)
         td(4)
-        absolute(7, "S")
+        td(5)
+        quantize_d(0, 1)
         cd(4)
         qd(4)
-        p1(1, 2)
-        store_1(1)
-        mask(7)
-        p1(2, 2)
-        store_1(2)
-        td(5)
+        absolute(7, "S")
+        group_d(0, 2)
         cd(5)
-        qd(5)
-        p1(3, 2)
-        store_1(3)
-        rest = {4: [(group_v, quantize_v, 0, 0), (group_d, quantize_d, 1, 0)], 5: [(group_v, quantize_v, 1, 0), (group_d, quantize_d, 1, 1)], 6: [(group_d, quantize_d, 1, 2)], 7: []}
-        late = []
-        for r in range(4, 8):
-            if r + 2 < 8:
-                td(r + 2)
-                cd(r + 2)
-            for n, (f, q, i, j) in enumerate(rest[r]):
-                f(i, j, "S" if (f, i, j) == (group_v, 1, 0) else "V")
-                for args in late:
-                    args[0](*args[1:])
-                late = [(q, i, j)]
-                if n == 0 and r + 2 < 8:
-                    qd(r + 2)
-            p1(r, 0)
-            p1(r, 1)
+        mask(7)
+        for r in range(1, 4):
             p1(r, 2)
+            store_1(r)
+        quantize_d(0, 2)
+        qd(5)
+        group_v(0, 0)
+        p1(4, 0)
+        p1(4, 1)
+        product_1(4, 2)
+        td(6)
+        td(7)
+        group_d(1, 0)
+        copy_1(4, 2, "S")
+        store_1(4)
+        cd(6)
+        cd(7)
+        qd(6)
+        quantize_v(0, 0)
+        quantize_d(1, 0)
+        qd(7)
+        for c in range(MC):
+            p1(5, c)
+        store_1(5)
+        group_half(("v", 1, 0), held["v", 1], slice(0, N), 0, "V")
+        group_half(("v", 1, 0), held["v", 1], slice(0, N), 1, "S")
+        group_d(1, 1)
+        quantize_v(1, 0)
+        group_d(1, 2)
+        quantize_d(1, 1)
+        for r in range(6, 8):
+            for c in range(MC):
+                p1(r, c)
             store_1(r)
         quantize_d(1, 2)
 

@@ -11,7 +11,6 @@ F32 = mybir.dt.float32
 BF16 = mybir.dt.bfloat16
 U32 = mybir.dt.uint32
 U8 = mybir.dt.uint8
-I32 = mybir.dt.int32
 E4M3 = mybir.dt.float8_e4m3fn_x4
 E5M2 = mybir.dt.float8_e5m2_x4
 ALU = mybir.AluOpType
@@ -23,24 +22,30 @@ N = 512
 DG = D // K
 TG = T // K
 MC = M // N
-ROWS = 6
-GROUPED = 3
-D_PARTS = ((0, 1), (2,))
+ROWS = 4 * DG
+PIECES = M // (2 * P)
+BLOCKS = M // P
+ROW_PARTS = ((0, 1), (2,))
+
+BIG_SLOTS = 10
+TURNED_BUFS = 6
+GROUPED_BUFS = 3
 
 
 def tile_blueboxlayer_pb_v_kernel(tc, Z, X, U, V, l1, mat, grad_out, out_0, out_1):
     nc = tc.nc
+    vector_copy, scalar_copy = nc.vector.tensor_copy, nc.scalar.copy
     with ExitStack() as ctx:
         const = ctx.enter_context(tc.tile_pool(name="const", bufs=1))
-        big = ctx.enter_context(tc.tile_pool(name="big", bufs=10))
+        big = ctx.enter_context(tc.tile_pool(name="big", bufs=BIG_SLOTS))
         keep = ctx.enter_context(tc.tile_pool(name="keep", bufs=1))
-        work = ctx.enter_context(tc.tile_pool(name="work", bufs=3))
+        work = ctx.enter_context(tc.tile_pool(name="work", bufs=GROUPED_BUFS))
         psum = ctx.enter_context(tc.psum_pool(name="psum", bufs=8))
         ctx.enter_context(tc.manual_schedule())
 
         thres = const.tile([P, 1], F32, name="thres")
-        raw = const.tile([1, 1], BF16, name="l1_raw")
-        column = const.tile([P, 1], F32, name="l1_column")
+        l1_raw = const.tile([1, 1], BF16, name="l1_raw")
+        l1_column = const.tile([P, 1], F32, name="l1_column")
         ident = const.tile([P, P], F32, name="ident")
         make_identity(nc, ident[:])
 
@@ -50,44 +55,10 @@ def tile_blueboxlayer_pb_v_kernel(tc, Z, X, U, V, l1, mat, grad_out, out_0, out_
         x_v = X.rearrange("(k p i) t -> k p i t", p=P, i=2)
         out_1v = out_1.rearrange("(g p j) m -> g p j m", g=DG, j=4)
         out_0v = out_0.rearrange("(b p) t -> p b t", p=P)
-        grads = [keep.tile([P, 4, T], BF16, name="grad%d" % g, align_bytes=256) for g in range(DG)]
-        dmat = grads
-        held = {}
 
-        def big_tile(key, shape, dtype):
-            if key not in held:
-                held[key] = big.tile(shape, dtype, name="%s%d" % key, tag="big", align_bytes=256)
-            return held[key]
-
-        def load_thres():
-            nc.scalar.dma_start(out=raw[:], in_=l1.rearrange("(a b) -> a b", a=1))
-            nc.vector.memset(column[:], 0.0)
-
-        def spread_thres():
-            nc.vector.tensor_copy(out=column[0:1, :], in_=raw[:])
-            bank = psum.tile([P, P], F32, name="bank_l1", tag="bank")
-            nc.tensor.transpose(bank[:], column[:].to_broadcast([P, P]), ident[:])
-            nc.vector.tensor_copy(out=thres[:], in_=bank[:, 0:1])
-
-        def load_mat(r, n=1):
-            g, j = divmod(r, 4)
-            t = big_tile(("mat", r // 2), [P, 2, T], F32)
-            nc.sync.dma_start(out=t[:, r % 2 : r % 2 + n, :], in_=mat_v[g, :, j : j + n, :])
-
-        def load_grad(r, n):
-            g, j = divmod(r, 4)
-            nc.sync.dma_start(out=grads[g][:, j : j + n, :], in_=grad_v[g, :, j : j + n, :])
-
-        def load_x(k):
-            t = big_tile(("x", k // 2), [P, 2, 2, T], BF16)
-            nc.sync.dma_start(out=t[:, k % 2], in_=x_v[k])
-
-        def load_v(g):
-            t = big_tile(("v", g), [P, 4, M], BF16)
-            nc.sync.dma_start(out=t[:], in_=v_v[g])
-
-        dt_codes = [keep.tile([P, TG * P], U32, name="dt_codes%d" % r, align_bytes=64) for r in range(4 * DG)]
-        dt_scales = [keep.tile([P, TG * P], U8, name="dt_scales%d" % r, align_bytes=64) for r in range(4 * DG)]
+        dmat = [keep.tile([P, 4, T], BF16, name="dmat%d" % g, align_bytes=256) for g in range(DG)]
+        dt_codes = [keep.tile([P, TG * P], U32, name="dt_codes%d" % r, align_bytes=64) for r in range(ROWS)]
+        dt_scales = [keep.tile([P, TG * P], U8, name="dt_scales%d" % r, align_bytes=64) for r in range(ROWS)]
         x_codes = [keep.tile([P, TG, N], U32, name="x_codes%d" % c, align_bytes=64) for c in range(MC)]
         x_scales = [keep.tile([P, TG, N], U8, name="x_scales%d" % c, align_bytes=64) for c in range(MC)]
         d_codes = [keep.tile([P, DG, N], U32, name="d_codes%d" % s, align_bytes=64) for s in range(TG)]
@@ -95,99 +66,105 @@ def tile_blueboxlayer_pb_v_kernel(tc, Z, X, U, V, l1, mat, grad_out, out_0, out_
         v_codes = [keep.tile([P, DG, N], U32, name="v_codes%d" % c, align_bytes=64) for c in range(MC)]
         v_scales = [keep.tile([P, DG, N], U8, name="v_scales%d" % c, align_bytes=64) for c in range(MC)]
 
-        def evac(engine, out, in_):
-            if engine == "S":
-                nc.scalar.copy(out=out, in_=in_)
-            else:
-                nc.vector.tensor_copy(out=out, in_=in_)
+        big_tiles, banks, turned, grouped = {}, {}, {}, {}
 
-        def absolute(r, engine):
-            row = held["mat", r // 2][:, r % 2, :]
-            if engine == "S":
-                nc.scalar.activation(out=row, in_=row, func=ABS)
-            else:
-                bits = row.bitcast(I32)
-                nc.vector.tensor_scalar(out=bits, in0=bits, scalar1=0x7FFFFFFF, scalar2=None, op0=ALU.bitwise_and)
+        def big_tile(kind, index, shape, dtype):
+            if (kind, index) not in big_tiles:
+                big_tiles[kind, index] = big.tile(shape, dtype, name="%s%d" % (kind, index), tag="big", align_bytes=256)
+            return big_tiles[kind, index]
+
+        def mat_row(r):
+            return big_tile("mat", r // 2, [P, 2, T], F32)[:, r % 2 : r % 2 + 1, :]
+
+        def x_piece(k):
+            return big_tile("x", k // 2, [P, 2, 2, T], BF16)[:, k % 2]
+
+        def load_mat(r):
+            nc.sync.dma_start(out=mat_row(r), in_=mat_v[r // 4, :, r % 4 : r % 4 + 1, :])
+
+        def load_grad(r, n):
+            g, j = divmod(r, 4)
+            nc.sync.dma_start(out=dmat[g][:, j : j + n, :], in_=grad_v[g, :, j : j + n, :])
+
+        def load_x(k):
+            nc.sync.dma_start(out=x_piece(k), in_=x_v[k])
+
+        def load_v(g):
+            nc.sync.dma_start(out=big_tile("v", g, [P, 4, M], BF16)[:], in_=v_v[g])
+
+        def absolute(r):
+            row = mat_row(r)[:, 0, :]
+            nc.scalar.activation(out=row, in_=row, func=ABS)
 
         def mask(r):
-            g, j = divmod(r, 4)
-            nc.vector.scalar_tensor_tensor(
-                out=dmat[g][:, j, :], in0=held["mat", r // 2][:, r % 2, :], scalar=thres[:, 0:1],
-                in1=grads[g][:, j, :], op0=ALU.is_gt, op1=ALU.mult)
+            row = dmat[r // 4][:, r % 4, :]
+            nc.vector.scalar_tensor_tensor(out=row, in0=mat_row(r)[:, 0, :], scalar=thres[:, 0:1], in1=row,
+                                           op0=ALU.is_gt, op1=ALU.mult)
 
-        banks, rows = {}, {}
+        def transpose_x(k):
+            words = x_piece(k).rearrange("p i t -> p (i t)").bitcast(F32)
+            for s in range(TG):
+                bank = psum.tile([P, 4, P], F32, name="bank_x", tag="bank")
+                for i in range(2):
+                    for u in range(2):
+                        first = i * (T // 2) + (K // 2) * s + u
+                        nc.tensor.transpose(bank[:, 2 * i + u, :], words[:, first : first + K // 2 - 1 : 2], ident[:])
+                banks["x", k, s] = bank
 
-        def transpose_x(k, s):
-            words = held["x", k // 2][:, k % 2].rearrange("p i t -> p (i t)").bitcast(F32)
-            bank = psum.tile([P, 4, P], F32, name="bank_x%d" % k, tag="bank")
-            for i in range(2):
-                for u in range(2):
-                    first = i * (T // 2) + 256 * s + u
-                    nc.tensor.transpose(bank[:, 2 * i + u, :], words[:, first : first + 255 : 2], ident[:])
-            banks[("x", k), s] = bank
+        def copy_x(k, engines):
+            for s, copy in enumerate(engines):
+                dest = work.tile([P, 2 * K], BF16, name="x_turned", tag="turned", bufs=TURNED_BUFS, align_bytes=64)
+                copy(out=dest[:].bitcast(F32).rearrange("q (p w) -> q p w", w=4),
+                     in_=banks["x", k, s][:].rearrange("q w p -> q p w"))
+                turned["x", k, s] = dest
 
-        def transpose_d(r, part):
-            g, j = divmod(r, 4)
-            words = dmat[g][:, j, :].bitcast(F32)
-            passes = D_PARTS[part]
-            bank = psum.tile([P, len(passes), 2, P], F32, name="bank_d%d" % r, tag="bank")
-            for n, s in enumerate(passes):
-                for u in range(2):
-                    first = 256 * s + u
-                    nc.tensor.transpose(bank[:, n, u, :], words[:, first : first + 255 : 2], ident[:])
-            banks[("d", r), part] = bank
-
-        def copy_x(k, s, engine):
-            t = work.tile([P, 2 * K], BF16, name="x%d_%d" % (k, s), tag="rows", bufs=ROWS, align_bytes=64)
-            evac(engine, t[:].bitcast(F32).rearrange("q (p w) -> q p w", w=4), banks[("x", k), s][:].rearrange("q w p -> q p w"))
-            rows["x", k, s] = t
-
-        def copy_d(r, part, engine):
-            n = len(D_PARTS[part])
-            t = work.tile([P, n * K], BF16, name="dt%d_%d" % (r, part), tag="rows", bufs=ROWS, align_bytes=64)
-            evac(engine, t[:].bitcast(F32).rearrange("q (s p u) -> q s p u", s=n, u=2),
-                 banks[("d", r), part][:].rearrange("q s u p -> q s p u"))
-            rows["d", r, part] = t
-
-        def quantize_x(k, s):
+        def quantize_x(k):
             half = slice((k % 2) * N // 2, (k % 2 + 1) * N // 2)
-            nc.vector.quantize_mx(out=x_codes[k // 2][:, s, half].bitcast(E4M3), scales=x_scales[k // 2][:, s, half],
-                                  in_=rows["x", k, s][:])
+            for s in range(TG):
+                nc.vector.quantize_mx(out=x_codes[k // 2][:, s, half].bitcast(E4M3),
+                                      scales=x_scales[k // 2][:, s, half], in_=turned["x", k, s][:])
 
-        def quantize_dt(r, part):
-            cols = slice(D_PARTS[part][0] * P, (D_PARTS[part][-1] + 1) * P)
-            nc.vector.quantize_mx(out=dt_codes[r][:, cols].bitcast(E5M2), scales=dt_scales[r][:, cols], in_=rows["d", r, part][:])
+        def transpose_row(r):
+            words = dmat[r // 4][:, r % 4, :].bitcast(F32)
+            for part, passes in enumerate(ROW_PARTS):
+                bank = psum.tile([P, len(passes), 2, P], F32, name="bank_row", tag="bank")
+                for n, s in enumerate(passes):
+                    for u in range(2):
+                        first = (K // 2) * s + u
+                        nc.tensor.transpose(bank[:, n, u, :], words[:, first : first + K // 2 - 1 : 2], ident[:])
+                banks["row", r, part] = bank
 
-        grouped = {}
+        def copy_row(r, copy=scalar_copy):
+            for part, passes in enumerate(ROW_PARTS):
+                dest = work.tile([P, len(passes) * K], BF16, name="row_turned", tag="turned", bufs=TURNED_BUFS,
+                                 align_bytes=64)
+                copy(out=dest[:].bitcast(F32).rearrange("q (s p u) -> q s p u", s=len(passes), u=2),
+                     in_=banks["row", r, part][:].rearrange("q s u p -> q s p u"))
+                turned["row", r, part] = dest
 
-        def group(key, src, cols, engine):
-            t = work.tile([P, N, 4], BF16, name="%s%d_%d" % key, tag="grouped", bufs=GROUPED, align_bytes=64)
-            evac(engine, t[:].rearrange("p (c i) j -> p c j i", i=4), src[:, :, cols].rearrange("p j (c i) -> p c j i", i=4))
-            grouped[key] = t
+        def quantize_row(r):
+            for part, passes in enumerate(ROW_PARTS):
+                cols = slice(passes[0] * P, (passes[-1] + 1) * P)
+                nc.vector.quantize_mx(out=dt_codes[r][:, cols].bitcast(E5M2), scales=dt_scales[r][:, cols],
+                                      in_=turned["row", r, part][:])
 
-        def group_half(key, src, cols, half, engine):
-            if key not in grouped:
-                grouped[key] = work.tile([P, N, 4], BF16, name="%s%d_%d" % key, tag="grouped", bufs=GROUPED, align_bytes=64)
-            part = slice(half * N // 2, (half + 1) * N // 2)
-            evac(engine, grouped[key][:, part].rearrange("p (c i) j -> p c j i", i=4),
-                 src[:, :, cols][:, :, part].rearrange("p j (c i) -> p c j i", i=4))
-
-        def group_d(g, s, engine="V"):
-            group(("d", g, s), dmat[g], slice(s * N, s * N + N), engine)
+        def interleave(kind, g, chunk, part=slice(0, N), copy=vector_copy):
+            if (kind, g, chunk) not in grouped:
+                grouped[kind, g, chunk] = work.tile([P, N, 4], BF16, name="grouped", tag="grouped", align_bytes=64)
+            source = dmat[g] if kind == "d" else big_tiles["v", g]
+            copy(out=grouped[kind, g, chunk][:, part].rearrange("p (c i) j -> p c j i", i=4),
+                 in_=source[:, :, chunk * N : chunk * N + N][:, :, part].rearrange("p j (c i) -> p c j i", i=4))
 
         def quantize_d(g, s):
             nc.vector.quantize_mx(out=d_codes[s][:, g, :].bitcast(E5M2), scales=d_scales[s][:, g, :],
                                   in_=grouped["d", g, s][:].rearrange("p n j -> p (n j)"))
 
-        def group_v(g, c, engine="V"):
-            group(("v", g, c), held["v", g], slice(c * N, c * N + N), engine)
-
         def quantize_v(g, c):
             nc.vector.quantize_mx(out=v_codes[c][:, g, :].bitcast(E4M3), scales=v_scales[c][:, g, :],
                                   in_=grouped["v", g, c][:].rearrange("p n j -> p (n j)"))
 
-        def product_1(r, c):
-            bank = psum.tile([P, N], F32, name="bank_r%d" % r, tag="bank")
+        def multiply_1(r, c):
+            bank = psum.tile([P, N], F32, name="bank_1", tag="bank")
             for s in range(TG):
                 cols = slice(s * P, s * P + P)
                 nc.tensor.matmul_mx(
@@ -196,186 +173,167 @@ def tile_blueboxlayer_pb_v_kernel(tc, Z, X, U, V, l1, mat, grad_out, out_0, out_
                     start=(s == 0), stop=(s == TG - 1))
             banks["out_1", r, c] = bank
 
-        def copy_1(r, c, engine):
-            stage = big_tile(("out_1", r // 2), [P, 2, M], F32)
-            evac(engine, stage[:, r % 2, c * N : c * N + N], banks["out_1", r, c][:])
+        def copy_1(r, c):
+            stage = big_tile("out_1_", r // 2, [P, 2, M], F32)
+            scalar_copy(out=stage[:, r % 2, c * N : c * N + N], in_=banks["out_1", r, c][:])
 
-        def store_1(r, n=1):
-            g, j = divmod(r, 4)
-            nc.sync.dma_start(out=out_1v[g, :, j : j + n, :], in_=held["out_1", r // 2][:, r % 2 : r % 2 + n, :])
+        def product_1(r, c):
+            multiply_1(r, c)
+            copy_1(r, c)
 
-        def product_0(b, s, engine):
-            stage = big_tile(("out_0", b // 2), [P, 2, T], F32)
+        def store_1(r):
+            nc.sync.dma_start(out=out_1v[r // 4, :, r % 4 : r % 4 + 1, :],
+                              in_=big_tiles["out_1_", r // 2][:, r % 2 : r % 2 + 1, :])
+
+        def product_0(b, s, copy):
+            stage = big_tile("out_0_", b // 2, [P, 2, T], F32)
             c, cols = b // 4, slice((b % 4) * P, (b % 4) * P + P)
-            bank = psum.tile([P, N], F32, name="bank_b%d" % b, tag="bank")
+            bank = psum.tile([P, N], F32, name="bank_0", tag="bank")
             for g in range(DG):
                 nc.tensor.matmul_mx(
                     out=bank[:], lhsT=v_codes[c][:, g, cols].bitcast(E4M3), lhsT_scale=v_scales[c][:, g, cols],
                     rhs=d_codes[s][:, g, :].bitcast(E5M2), rhs_scale=d_scales[s][:, g, :],
                     start=(g == 0), stop=(g == DG - 1))
-            evac(engine, stage[:, b % 2, s * N : s * N + N], bank[:])
+            copy(out=stage[:, b % 2, s * N : s * N + N], in_=bank[:])
 
-        def store_0(b, n=1, toks=slice(0, T)):
-            nc.sync.dma_start(out=out_0v[:, b : b + n, toks], in_=held["out_0", b // 2][:, b % 2 : b % 2 + n, toks])
+        def store_0(b):
+            nc.sync.dma_start(out=out_0v[:, b : b + 1, :], in_=big_tiles["out_0_", b // 2][:, b % 2 : b % 2 + 1, :])
 
-
-        load_thres()
-        load_mat(0)
-        load_grad(0, 2)
-        load_x(0)
-        load_mat(1)
-        load_x(1)
-        load_mat(2)
-        load_grad(2, 2)
-        load_mat(3)
-        for k in range(2, 6):
+        nc.scalar.dma_start(out=l1_raw[:], in_=l1.rearrange("(a b) -> a b", a=1))
+        nc.vector.memset(l1_column[:], 0.0)
+        for r in range(4):
+            load_mat(r)
+            load_grad(r, 1)
+            if r < 2:
+                load_x(r)
+        for k in range(2, PIECES):
             load_x(k)
-        for r in range(4, 8, 2):
+        for r in range(4, ROWS, 2):
             load_mat(r)
             load_grad(r, 2)
             load_mat(r + 1)
-        load_v(0)
-        load_v(1)
+        for g in range(DG):
+            load_v(g)
 
-        def tx(k):
-            for s in range(TG):
-                transpose_x(k, s)
+        vector_copy(out=l1_column[0:1, :], in_=l1_raw[:])
+        bank_l1 = psum.tile([P, P], F32, name="bank_l1", tag="bank")
+        nc.tensor.transpose(bank_l1[:], l1_column[:].to_broadcast([P, P]), ident[:])
+        vector_copy(out=thres[:], in_=bank_l1[:, 0:1])
 
-        def cx(k, engines):
-            for s in range(TG):
-                copy_x(k, s, engines[s])
-
-        def qx(k):
-            for s in range(TG):
-                quantize_x(k, s)
-
-        def td(r):
-            for part in range(2):
-                transpose_d(r, part)
-
-        def cd(r, engines="SS"):
-            for part in range(2):
-                copy_d(r, part, engines[part])
-
-        def qd(r):
-            for part in range(2):
-                quantize_dt(r, part)
-
-        def p1(r, c, engine="S"):
-            product_1(r, c)
-            copy_1(r, c, engine)
-
-        spread_thres()
-        absolute(0, "S")
+        absolute(0)
         mask(0)
-        tx(0)
-        cx(0, "SVV")
-        td(0)
-        absolute(1, "S")
-        qx(0)
-        cd(0, "SS")
-        tx(1)
+        transpose_x(0)
+        copy_x(0, (scalar_copy, vector_copy, vector_copy))
+        transpose_row(0)
+        absolute(1)
+        quantize_x(0)
+        copy_row(0)
+        transpose_x(1)
         mask(1)
-        qd(0)
-        cx(1, "SSS")
-        td(1)
-        qx(1)
-        absolute(2, "S")
-        cd(1, "VV")
-        qd(1)
+        quantize_row(0)
+        copy_x(1, (scalar_copy,) * TG)
+        transpose_row(1)
+        quantize_x(1)
+        absolute(2)
+        copy_row(1, vector_copy)
+        quantize_row(1)
         mask(2)
-        product_1(0, 0)
-        product_1(1, 0)
-        absolute(3, "S")
-        copy_1(0, 0, "S")
-        copy_1(1, 0, "S")
+        multiply_1(0, 0)
+        multiply_1(1, 0)
+        absolute(3)
+        copy_1(0, 0)
+        copy_1(1, 0)
         mask(3)
-        td(2)
-        tx(2)
-        cd(2, "SS")
-        cx(2, "SSS")
-        group_d(0, 0)
-        qd(2)
-        tx(3)
-        cx(3, "SSS")
-        qx(2)
+
+        transpose_row(2)
+        transpose_x(2)
+        copy_row(2)
+        copy_x(2, (scalar_copy,) * TG)
+        interleave("d", 0, 0)
+        quantize_row(2)
+        transpose_x(3)
+        copy_x(3, (scalar_copy,) * TG)
+        quantize_x(2)
         quantize_d(0, 0)
-        td(3)
-        tx(4)
-        qx(3)
-        cd(3, "SS")
-        cx(4, "SSS")
-        tx(5)
-        qd(3)
-        qx(4)
-        absolute(4, "S")
-        cx(5, "VVV")
-        qx(5)
+        transpose_row(3)
+        transpose_x(4)
+        quantize_x(3)
+        copy_row(3)
+        copy_x(4, (scalar_copy,) * TG)
+        transpose_x(5)
+        quantize_row(3)
+        interleave("d", 0, 1, slice(0, N // 2))
+        quantize_x(4)
+        absolute(4)
+        copy_x(5, (vector_copy,) * TG)
+        quantize_x(5)
 
         mask(4)
-        p1(0, 1)
-        absolute(5, "S")
+        product_1(0, 1)
+        absolute(5)
         mask(5)
-        p1(1, 1)
-        p1(2, 0)
-        absolute(6, "S")
-        group_d(0, 1)
-        p1(2, 1)
-        p1(3, 0)
+        product_1(1, 1)
+        product_1(2, 0)
+        absolute(6)
+        interleave("d", 0, 1, slice(N // 2, N))
+        product_1(2, 1)
+        product_1(3, 0)
         mask(6)
-        p1(3, 1)
-        p1(0, 2)
+        product_1(3, 1)
+        product_1(0, 2)
         store_1(0)
-        td(4)
-        td(5)
+        transpose_row(4)
+        transpose_row(5)
         quantize_d(0, 1)
-        cd(4)
-        qd(4)
-        absolute(7, "S")
-        group_d(0, 2)
-        cd(5)
+        copy_row(4)
+        quantize_row(4)
+        absolute(7)
+        interleave("d", 0, 2)
+        copy_row(5)
         mask(7)
         for r in range(1, 4):
-            p1(r, 2)
+            product_1(r, 2)
             store_1(r)
+
         quantize_d(0, 2)
-        qd(5)
-        group_v(0, 0)
-        p1(4, 0)
-        p1(4, 1)
-        product_1(4, 2)
-        td(6)
-        td(7)
-        group_d(1, 0)
-        copy_1(4, 2, "S")
+        quantize_row(5)
+        interleave("v", 0, 0)
+        product_1(4, 0)
+        product_1(4, 1)
+        multiply_1(4, 2)
+        transpose_row(6)
+        transpose_row(7)
+        interleave("d", 1, 0)
+        copy_1(4, 2)
         store_1(4)
-        cd(6)
-        cd(7)
-        qd(6)
+        copy_row(6)
+        copy_row(7)
+        quantize_row(6)
         quantize_v(0, 0)
         quantize_d(1, 0)
-        qd(7)
+        quantize_row(7)
         for c in range(MC):
-            p1(5, c)
+            product_1(5, c)
         store_1(5)
-        group_half(("v", 1, 0), held["v", 1], slice(0, N), 0, "V")
-        group_half(("v", 1, 0), held["v", 1], slice(0, N), 1, "S")
-        group_d(1, 1)
+        interleave("v", 1, 0, slice(0, N // 2))
+        interleave("v", 1, 0, slice(N // 2, N), scalar_copy)
+        interleave("d", 1, 1)
         quantize_v(1, 0)
-        group_d(1, 2)
+        interleave("d", 1, 2)
         quantize_d(1, 1)
-        for r in range(6, 8):
+        for r in range(6, ROWS):
             for c in range(MC):
-                p1(r, c)
+                product_1(r, c)
             store_1(r)
         quantize_d(1, 2)
 
-        for b in range(12):
+        for b in range(BLOCKS):
             c, n = divmod(b, 4)
-            if n < 2 and c < 2:
-                group_v(n, c + 1)
-            if 0 < n < 3 and c < 2:
+            next_chunk = c + 1 < MC
+            if next_chunk and n < DG:
+                interleave("v", n, c + 1)
+            if next_chunk and 0 < n <= DG:
                 quantize_v(n - 1, c + 1)
             for s in range(TG):
-                product_0(b, s, "S" if (n < 2 and c < 2) or (b + s) % 2 == 0 else "V")
+                product_0(b, s, scalar_copy if (next_chunk and n < DG) or (b + s) % 2 == 0 else vector_copy)
             store_0(b)

@@ -9,6 +9,7 @@ BYTES = 2 * (M * T + D * M + D * T) + 4 * (D * T + M * T + D * M) + 2
 
 F32 = mybir.dt.float32
 BF16 = mybir.dt.bfloat16
+I32 = mybir.dt.int32
 U32 = mybir.dt.uint32
 U8 = mybir.dt.uint8
 E4M3 = mybir.dt.float8_e4m3fn_x4
@@ -24,8 +25,7 @@ TG = T // K
 MC = M // N
 ROWS = 4 * DG
 PIECES = M // (2 * P)
-BLOCKS = M // P
-ROW_PARTS = ((0, 1), (2,))
+NO_SIGN = 0x7FFFFFFF
 
 BIG_SLOTS = 10
 TURNED_BUFS = 6
@@ -54,17 +54,17 @@ def tile_blueboxlayer_pb_v_kernel(tc, Z, X, U, V, l1, mat, grad_out, out_0, out_
         v_v = V.rearrange("(g p j) m -> g p j m", g=DG, j=4)
         x_v = X.rearrange("(k p i) t -> k p i t", p=P, i=2)
         out_1v = out_1.rearrange("(g p j) m -> g p j m", g=DG, j=4)
-        out_0v = out_0.rearrange("(b p) t -> p b t", p=P)
+        out_0v = out_0.rearrange("(k p i) t -> k p i t", p=P, i=2)
 
         dmat = [keep.tile([P, 4, T], BF16, name="dmat%d" % g, align_bytes=256) for g in range(DG)]
-        dt_codes = [keep.tile([P, TG * P], U32, name="dt_codes%d" % r, align_bytes=64) for r in range(ROWS)]
-        dt_scales = [keep.tile([P, TG * P], U8, name="dt_scales%d" % r, align_bytes=64) for r in range(ROWS)]
+        dt_codes = keep.tile([P, ROWS * TG * P], U32, name="dt_codes", align_bytes=64)
+        dt_scales = keep.tile([P, ROWS * TG * P], U8, name="dt_scales", align_bytes=64)
         x_codes = [keep.tile([P, TG, N], U32, name="x_codes%d" % c, align_bytes=64) for c in range(MC)]
         x_scales = [keep.tile([P, TG, N], U8, name="x_scales%d" % c, align_bytes=64) for c in range(MC)]
         d_codes = [keep.tile([P, DG, N], U32, name="d_codes%d" % s, align_bytes=64) for s in range(TG)]
         d_scales = [keep.tile([P, DG, N], U8, name="d_scales%d" % s, align_bytes=64) for s in range(TG)]
-        v_codes = [keep.tile([P, DG, N], U32, name="v_codes%d" % c, align_bytes=64) for c in range(MC)]
-        v_scales = [keep.tile([P, DG, N], U8, name="v_scales%d" % c, align_bytes=64) for c in range(MC)]
+        v_codes = [keep.tile([P, DG, 2 * P], U32, name="v_codes%d" % k, align_bytes=64) for k in range(PIECES)]
+        v_scales = [keep.tile([P, DG, 2 * P], U8, name="v_scales%d" % k, align_bytes=64) for k in range(PIECES)]
 
         big_tiles, banks, turned, grouped = {}, {}, {}, {}
 
@@ -73,18 +73,20 @@ def tile_blueboxlayer_pb_v_kernel(tc, Z, X, U, V, l1, mat, grad_out, out_0, out_
                 big_tiles[kind, index] = big.tile(shape, dtype, name="%s%d" % (kind, index), tag="big", align_bytes=256)
             return big_tiles[kind, index]
 
-        def mat_row(r):
-            return big_tile("mat", r // 2, [P, 2, T], F32)[:, r % 2 : r % 2 + 1, :]
+        def mat_rows(r, n=1):
+            return big_tile("mat", r // 2, [P, 2, T], F32)[:, r % 2 : r % 2 + n, :]
+
+        def grad_row(r, n=1):
+            return big_tile("grad", r // 4, [P, 4, T], BF16)[:, r % 4 : r % 4 + n, :]
 
         def x_piece(k):
             return big_tile("x", k // 2, [P, 2, 2, T], BF16)[:, k % 2]
 
-        def load_mat(r):
-            nc.sync.dma_start(out=mat_row(r), in_=mat_v[r // 4, :, r % 4 : r % 4 + 1, :])
+        def load_mat(r, n=1):
+            nc.sync.dma_start(out=mat_rows(r, n), in_=mat_v[r // 4, :, r % 4 : r % 4 + n, :])
 
-        def load_grad(r, n):
-            g, j = divmod(r, 4)
-            nc.sync.dma_start(out=dmat[g][:, j : j + n, :], in_=grad_v[g, :, j : j + n, :])
+        def load_grad(r, n=1):
+            nc.sync.dma_start(out=grad_row(r, n), in_=grad_v[r // 4, :, r % 4 : r % 4 + n, :])
 
         def load_x(k):
             nc.sync.dma_start(out=x_piece(k), in_=x_v[k])
@@ -92,14 +94,21 @@ def tile_blueboxlayer_pb_v_kernel(tc, Z, X, U, V, l1, mat, grad_out, out_0, out_
         def load_v(g):
             nc.sync.dma_start(out=big_tile("v", g, [P, 4, M], BF16)[:], in_=v_v[g])
 
-        def absolute(r):
-            row = mat_row(r)[:, 0, :]
+        def absolute(r, cols=slice(0, T)):
+            row = mat_rows(r)[:, 0, cols]
             nc.scalar.activation(out=row, in_=row, func=ABS)
 
+        def absolute_on_vector(r, cols=slice(0, T)):
+            bits = mat_rows(r)[:, 0, cols].bitcast(I32)
+            nc.vector.tensor_single_scalar(out=bits, in_=bits, scalar=NO_SIGN, op=ALU.bitwise_and)
+
         def mask(r):
-            row = dmat[r // 4][:, r % 4, :]
-            nc.vector.scalar_tensor_tensor(out=row, in0=mat_row(r)[:, 0, :], scalar=thres[:, 0:1], in1=row,
-                                           op0=ALU.is_gt, op1=ALU.mult)
+            for u in range(2):
+                pairs = "p (s q u e) -> p u s q e"
+                nc.vector.scalar_tensor_tensor(
+                    out=dmat[r // 4][:, r % 4, :].rearrange("p (s u q e) -> p u s q e", s=TG, u=2, e=2)[:, u],
+                    in0=mat_rows(r)[:, 0, :].rearrange(pairs, s=TG, u=2, e=2)[:, u], scalar=thres[:, 0:1],
+                    in1=grad_row(r)[:, 0, :].rearrange(pairs, s=TG, u=2, e=2)[:, u], op0=ALU.is_gt, op1=ALU.mult)
 
         def transpose_x(k):
             words = x_piece(k).rearrange("p i t -> p (i t)").bitcast(F32)
@@ -111,229 +120,256 @@ def tile_blueboxlayer_pb_v_kernel(tc, Z, X, U, V, l1, mat, grad_out, out_0, out_
                         nc.tensor.transpose(bank[:, 2 * i + u, :], words[:, first : first + K // 2 - 1 : 2], ident[:])
                 banks["x", k, s] = bank
 
-        def copy_x(k, engines):
-            for s, copy in enumerate(engines):
+        def copy_x(k, passes=range(TG), copy=scalar_copy):
+            for s in passes:
                 dest = work.tile([P, 2 * K], BF16, name="x_turned", tag="turned", bufs=TURNED_BUFS, align_bytes=64)
                 copy(out=dest[:].bitcast(F32).rearrange("q (p w) -> q p w", w=4),
                      in_=banks["x", k, s][:].rearrange("q w p -> q p w"))
                 turned["x", k, s] = dest
 
-        def quantize_x(k):
+        def quantize_x(k, passes=range(TG)):
             half = slice((k % 2) * N // 2, (k % 2 + 1) * N // 2)
-            for s in range(TG):
+            for s in passes:
                 nc.vector.quantize_mx(out=x_codes[k // 2][:, s, half].bitcast(E4M3),
                                       scales=x_scales[k // 2][:, s, half], in_=turned["x", k, s][:])
 
-        def transpose_row(r):
-            words = dmat[r // 4][:, r % 4, :].bitcast(F32)
-            for part, passes in enumerate(ROW_PARTS):
-                bank = psum.tile([P, len(passes), 2, P], F32, name="bank_row", tag="bank")
-                for n, s in enumerate(passes):
+        def bank_parts(r, n):
+            return [range(a, min(a + 2, TG * (r + n))) for a in range(TG * r, TG * (r + n), 2)]
+
+        def transpose_rows(r, n=1):
+            for part in bank_parts(r, n):
+                bank = psum.tile([P, len(part), 2, P], F32, name="bank_row", tag="bank")
+                for place, a in enumerate(part):
+                    row, s = divmod(a, TG)
+                    words = dmat[row // 4][:, row % 4, :].bitcast(F32)
                     for u in range(2):
-                        first = (K // 2) * s + u
-                        nc.tensor.transpose(bank[:, n, u, :], words[:, first : first + K // 2 - 1 : 2], ident[:])
-                banks["row", r, part] = bank
+                        first = (2 * s + u) * P
+                        nc.tensor.transpose(bank[:, place, u, :], words[:, first : first + P], ident[:])
+                banks["row", part[0]] = bank
 
-        def copy_row(r, copy=scalar_copy):
-            for part, passes in enumerate(ROW_PARTS):
-                dest = work.tile([P, len(passes) * K], BF16, name="row_turned", tag="turned", bufs=TURNED_BUFS,
+        def copy_rows(r, n=1, copy=scalar_copy, which=slice(None)):
+            for part in bank_parts(r, n)[which]:
+                dest = work.tile([P, len(part) * K], BF16, name="row_turned", tag="turned", bufs=TURNED_BUFS,
                                  align_bytes=64)
-                copy(out=dest[:].bitcast(F32).rearrange("q (s p u) -> q s p u", s=len(passes), u=2),
-                     in_=banks["row", r, part][:].rearrange("q s u p -> q s p u"))
-                turned["row", r, part] = dest
+                copy(out=dest[:].bitcast(F32).rearrange("q (s p u) -> q s p u", s=len(part), u=2),
+                     in_=banks["row", part[0]][:].rearrange("q s u p -> q s p u"))
+                turned["row", part[0]] = dest
 
-        def quantize_row(r):
-            for part, passes in enumerate(ROW_PARTS):
-                cols = slice(passes[0] * P, (passes[-1] + 1) * P)
-                nc.vector.quantize_mx(out=dt_codes[r][:, cols].bitcast(E5M2), scales=dt_scales[r][:, cols],
-                                      in_=turned["row", r, part][:])
+        def quantize_rows(r, n=1, which=slice(None)):
+            for part in bank_parts(r, n)[which]:
+                cols = slice(part[0] * P, (part[-1] + 1) * P)
+                nc.vector.quantize_mx(out=dt_codes[:, cols].bitcast(E5M2), scales=dt_scales[:, cols],
+                                      in_=turned["row", part[0]][:])
 
-        def interleave(kind, g, chunk, part=slice(0, N), copy=vector_copy):
-            if (kind, g, chunk) not in grouped:
-                grouped[kind, g, chunk] = work.tile([P, N, 4], BF16, name="grouped", tag="grouped", align_bytes=64)
-            source = dmat[g] if kind == "d" else big_tiles["v", g]
-            copy(out=grouped[kind, g, chunk][:, part].rearrange("p (c i) j -> p c j i", i=4),
-                 in_=source[:, :, chunk * N : chunk * N + N][:, :, part].rearrange("p j (c i) -> p c j i", i=4))
+        def interleave_d(g, s, part=slice(0, N), copy=vector_copy):
+            if ("d", g, s) not in grouped:
+                grouped["d", g, s] = work.tile([P, N, 4], BF16, name="d_grouped", tag="grouped", align_bytes=64)
+            copy(out=grouped["d", g, s][:, part].rearrange("p (c i) j -> p c j i", i=4),
+                 in_=dmat[g][:, :, s * N : s * N + N][:, :, part].rearrange("p j (c i) -> p c j i", i=4))
+
+        def interleave_v(g, k, copy=vector_copy):
+            grouped["v", g, k] = work.tile([P, 2 * P, 4], BF16, name="v_grouped", tag="grouped", align_bytes=64)
+            copy(out=grouped["v", g, k][:].rearrange("p (i c h) j -> p c j i h", i=2, h=2),
+                 in_=big_tiles["v", g][:, :, 2 * P * k : 2 * P * (k + 1)].rearrange("p j (c h i) -> p c j i h", h=2, i=2))
 
         def quantize_d(g, s):
             nc.vector.quantize_mx(out=d_codes[s][:, g, :].bitcast(E5M2), scales=d_scales[s][:, g, :],
                                   in_=grouped["d", g, s][:].rearrange("p n j -> p (n j)"))
 
-        def quantize_v(g, c):
-            nc.vector.quantize_mx(out=v_codes[c][:, g, :].bitcast(E4M3), scales=v_scales[c][:, g, :],
-                                  in_=grouped["v", g, c][:].rearrange("p n j -> p (n j)"))
+        def quantize_v(g, k):
+            nc.vector.quantize_mx(out=v_codes[k][:, g, :].bitcast(E4M3), scales=v_scales[k][:, g, :],
+                                  in_=grouped["v", g, k][:].rearrange("p n j -> p (n j)"))
 
         def multiply_1(r, c):
             bank = psum.tile([P, N], F32, name="bank_1", tag="bank")
             for s in range(TG):
-                cols = slice(s * P, s * P + P)
+                cols = slice((TG * r + s) * P, (TG * r + s + 1) * P)
                 nc.tensor.matmul_mx(
-                    out=bank[:], lhsT=dt_codes[r][:, cols].bitcast(E5M2), lhsT_scale=dt_scales[r][:, cols],
+                    out=bank[:], lhsT=dt_codes[:, cols].bitcast(E5M2), lhsT_scale=dt_scales[:, cols],
                     rhs=x_codes[c][:, s, :].bitcast(E4M3), rhs_scale=x_scales[c][:, s, :],
                     start=(s == 0), stop=(s == TG - 1))
             banks["out_1", r, c] = bank
 
-        def copy_1(r, c):
+        def copy_1(r, c, copy=scalar_copy):
             stage = big_tile("out_1_", r // 2, [P, 2, M], F32)
-            scalar_copy(out=stage[:, r % 2, c * N : c * N + N], in_=banks["out_1", r, c][:])
+            copy(out=stage[:, r % 2, c * N : c * N + N], in_=banks["out_1", r, c][:])
 
-        def product_1(r, c):
+        def product_1(r, c, copy=scalar_copy):
             multiply_1(r, c)
-            copy_1(r, c)
+            copy_1(r, c, copy)
 
-        def store_1(r):
-            nc.sync.dma_start(out=out_1v[r // 4, :, r % 4 : r % 4 + 1, :],
-                              in_=big_tiles["out_1_", r // 2][:, r % 2 : r % 2 + 1, :])
+        def store_1(r, n=1):
+            nc.sync.dma_start(out=out_1v[r // 4, :, r % 4 : r % 4 + n, :],
+                              in_=big_tiles["out_1_", r // 2][:, r % 2 : r % 2 + n, :])
 
-        def product_0(b, s, copy):
-            stage = big_tile("out_0_", b // 2, [P, 2, T], F32)
-            c, cols = b // 4, slice((b % 4) * P, (b % 4) * P + P)
+        def product_0(k, i, s, copy):
+            stage = big_tile("out_0_", k, [P, 2, T], F32)
+            cols = slice(i * P, i * P + P)
             bank = psum.tile([P, N], F32, name="bank_0", tag="bank")
             for g in range(DG):
                 nc.tensor.matmul_mx(
-                    out=bank[:], lhsT=v_codes[c][:, g, cols].bitcast(E4M3), lhsT_scale=v_scales[c][:, g, cols],
+                    out=bank[:], lhsT=v_codes[k][:, g, cols].bitcast(E4M3), lhsT_scale=v_scales[k][:, g, cols],
                     rhs=d_codes[s][:, g, :].bitcast(E5M2), rhs_scale=d_scales[s][:, g, :],
                     start=(g == 0), stop=(g == DG - 1))
-            copy(out=stage[:, b % 2, s * N : s * N + N], in_=bank[:])
+            copy(out=stage[:, i, s * N : s * N + N].rearrange("p (q u e) -> p q u e", u=2, e=2),
+                 in_=bank[:].rearrange("p (u q e) -> p q u e", u=2, e=2))
 
-        def store_0(b):
-            nc.sync.dma_start(out=out_0v[:, b : b + 1, :], in_=big_tiles["out_0_", b // 2][:, b % 2 : b % 2 + 1, :])
+        def store_0(k, halves):
+            nc.sync.dma_start(out=out_0v[k, :, halves, :], in_=big_tiles["out_0_", k][:, halves, :])
 
         nc.scalar.dma_start(out=l1_raw[:], in_=l1.rearrange("(a b) -> a b", a=1))
         nc.vector.memset(l1_column[:], 0.0)
-        for r in range(4):
-            load_mat(r)
-            load_grad(r, 1)
-            if r < 2:
-                load_x(r)
-        for k in range(2, PIECES):
-            load_x(k)
-        for r in range(4, ROWS, 2):
-            load_mat(r)
-            load_grad(r, 2)
-            load_mat(r + 1)
-        for g in range(DG):
-            load_v(g)
+        load_mat(0, 1)
+        load_grad(0, 1)
+        load_mat(1, 1)
+        load_grad(1, 1)
+        load_x(0)
+        load_x(1)
+        load_x(2)
+        load_x(3)
+        load_mat(2, 1)
+        load_grad(2, 1)
+        load_mat(3, 1)
+        load_grad(3, 1)
+        load_x(4)
+        load_x(5)
+        big_tile("out_1_", 0, [P, 2, M], F32)
+        load_mat(4, 1)
+        load_grad(4, 2)
+        load_mat(5, 1)
+        load_mat(6, 1)
+        load_grad(6, 2)
+        load_mat(7, 1)
 
         vector_copy(out=l1_column[0:1, :], in_=l1_raw[:])
         bank_l1 = psum.tile([P, P], F32, name="bank_l1", tag="bank")
         nc.tensor.transpose(bank_l1[:], l1_column[:].to_broadcast([P, P]), ident[:])
         vector_copy(out=thres[:], in_=bank_l1[:, 0:1])
 
-        absolute(0)
+        absolute_on_vector(0)
         mask(0)
-        transpose_x(0)
-        copy_x(0, (scalar_copy, vector_copy, vector_copy))
-        transpose_row(0)
-        absolute(1)
-        quantize_x(0)
-        copy_row(0)
-        transpose_x(1)
+        absolute_on_vector(1)
+        transpose_rows(0)
         mask(1)
-        quantize_row(0)
-        copy_x(1, (scalar_copy,) * TG)
-        transpose_row(1)
+        copy_rows(0)
+        transpose_x(0)
+        copy_x(0)
+        quantize_rows(0)
+        transpose_x(1)
+        quantize_x(0)
+        copy_x(1)
+        transpose_x(2)
         quantize_x(1)
-        absolute(2)
-        copy_row(1, vector_copy)
-        quantize_row(1)
+        copy_x(2)
+        transpose_x(3)
+        transpose_rows(1)
+        quantize_x(2)
+        copy_x(3)
+        absolute_on_vector(2)
+        copy_rows(1)
+        quantize_x(3)
+        quantize_rows(1)
         mask(2)
         multiply_1(0, 0)
-        multiply_1(1, 0)
+        multiply_1(0, 1)
         absolute(3)
         copy_1(0, 0)
-        copy_1(1, 0)
+        copy_1(0, 1)
         mask(3)
-
-        transpose_row(2)
-        transpose_x(2)
-        copy_row(2)
-        copy_x(2, (scalar_copy,) * TG)
-        interleave("d", 0, 0)
-        quantize_row(2)
-        transpose_x(3)
-        copy_x(3, (scalar_copy,) * TG)
-        quantize_x(2)
-        quantize_d(0, 0)
-        transpose_row(3)
+        load_v(0)
+        load_v(1)
+        product_1(1, 0)
+        transpose_rows(2)
         transpose_x(4)
-        quantize_x(3)
-        copy_row(3)
-        copy_x(4, (scalar_copy,) * TG)
+        multiply_1(1, 1)
+        copy_rows(2)
+        copy_x(4)
+        interleave_d(0, 0)
+        quantize_rows(2)
         transpose_x(5)
-        quantize_row(3)
-        interleave("d", 0, 1, slice(0, N // 2))
+        transpose_rows(3)
+        absolute_on_vector(4)
         quantize_x(4)
-        absolute(4)
-        copy_x(5, (vector_copy,) * TG)
+        copy_x(5)
+        copy_rows(3)
         quantize_x(5)
-
         mask(4)
-        product_1(0, 1)
+        quantize_rows(3)
+        quantize_d(0, 0)
+        copy_1(1, 1)
+        multiply_1(2, 0)
+        multiply_1(2, 1)
         absolute(5)
         mask(5)
-        product_1(1, 1)
-        product_1(2, 0)
+        copy_1(2, 0)
         absolute(6)
-        interleave("d", 0, 1, slice(N // 2, N))
-        product_1(2, 1)
-        product_1(3, 0)
+        interleave_d(0, 1, slice(0, N // 2))
         mask(6)
-        product_1(3, 1)
+        copy_1(2, 1)
         product_1(0, 2)
         store_1(0)
-        transpose_row(4)
-        transpose_row(5)
-        quantize_d(0, 1)
-        copy_row(4)
-        quantize_row(4)
-        absolute(7)
-        interleave("d", 0, 2)
-        copy_row(5)
+        multiply_1(1, 2)
+        multiply_1(2, 2)
+        multiply_1(3, 0)
+        transpose_rows(4, 2)
+        copy_1(1, 2)
+        store_1(1)
+        copy_rows(4, 2)
+        absolute_on_vector(7)
+        quantize_rows(4, 2)
         mask(7)
-        for r in range(1, 4):
-            product_1(r, 2)
-            store_1(r)
-
-        quantize_d(0, 2)
-        quantize_row(5)
-        interleave("v", 0, 0)
-        product_1(4, 0)
-        product_1(4, 1)
-        multiply_1(4, 2)
-        transpose_row(6)
-        transpose_row(7)
-        interleave("d", 1, 0)
-        copy_1(4, 2)
-        store_1(4)
-        copy_row(6)
-        copy_row(7)
-        quantize_row(6)
-        quantize_v(0, 0)
-        quantize_d(1, 0)
-        quantize_row(7)
+        interleave_d(0, 1, slice(N // 2, N))
+        interleave_d(0, 2)
+        quantize_d(0, 1)
+        copy_1(2, 2)
+        store_1(2)
+        copy_1(3, 0)
+        product_1(3, 1)
+        product_1(3, 2)
+        store_1(3)
         for c in range(MC):
-            product_1(5, c)
+            product_1(4, c)
+        store_1(4)
+        quantize_d(0, 2)
+        multiply_1(5, 0)
+        transpose_rows(6, 2)
+        copy_rows(6, 2)
+        copy_1(5, 0)
+        interleave_d(1, 0, slice(0, N // 2))
+        quantize_rows(6, 2)
+        interleave_d(1, 0, slice(N // 2, N))
+        interleave_d(1, 1)
+        quantize_d(1, 0)
+        product_1(5, 1)
+        product_1(5, 2)
         store_1(5)
-        interleave("v", 1, 0, slice(0, N // 2))
-        interleave("v", 1, 0, slice(N // 2, N), scalar_copy)
-        interleave("d", 1, 1)
-        quantize_v(1, 0)
-        interleave("d", 1, 2)
+        interleave_v(0, 0, scalar_copy)
         quantize_d(1, 1)
-        for r in range(6, ROWS):
-            for c in range(MC):
-                product_1(r, c)
-            store_1(r)
+        for c in range(MC):
+            product_1(6, c)
+        store_1(6)
+        quantize_v(0, 0)
+        interleave_v(1, 0, scalar_copy)
+        interleave_d(1, 2)
+        quantize_v(1, 0)
         quantize_d(1, 2)
-
-        for b in range(BLOCKS):
-            c, n = divmod(b, 4)
-            next_chunk = c + 1 < MC
-            if next_chunk and n < DG:
-                interleave("v", n, c + 1)
-            if next_chunk and 0 < n <= DG:
-                quantize_v(n - 1, c + 1)
-            for s in range(TG):
-                product_0(b, s, scalar_copy if (next_chunk and n < DG) or (b + s) % 2 == 0 else vector_copy)
-            store_0(b)
+        for c in range(MC):
+            product_1(7, c)
+        store_1(7)
+        for k in range(PIECES):
+            more = k + 1 < PIECES
+            if more:
+                interleave_v(0, k + 1)
+                interleave_v(1, k + 1)
+                quantize_v(0, k + 1)
+                quantize_v(1, k + 1)
+            if k == 0:
+                for i, s in ((0, 0), (1, 0), (0, 1), (0, 2), (1, 1), (1, 2)):
+                    product_0(k, i, s, scalar_copy)
+                    if s == TG - 1:
+                        store_0(k, slice(i, i + 1))
+                continue
+            for i in range(2):
+                for s in range(TG):
+                    product_0(k, i, s, vector_copy if (i == 1 and s != 1) or (not more and s == 1) else scalar_copy)
+                store_0(k, slice(i, i + 1))

@@ -76,9 +76,6 @@ def tile_blueboxlayer_pb_v_kernel(tc, Z, X, U, V, l1, mat, grad_out, out_0, out_
         def mat_rows(r, n=1):
             return big_tile("mat", r // 2, [P, 2, T], F32)[:, r % 2 : r % 2 + n, :]
 
-        def grad_row(r, n=1):
-            return big_tile("grad", r // 4, [P, 4, T], BF16)[:, r % 4 : r % 4 + n, :]
-
         def x_piece(k):
             return big_tile("x", k // 2, [P, 2, 2, T], BF16)[:, k % 2]
 
@@ -86,7 +83,8 @@ def tile_blueboxlayer_pb_v_kernel(tc, Z, X, U, V, l1, mat, grad_out, out_0, out_
             nc.sync.dma_start(out=mat_rows(r, n), in_=mat_v[r // 4, :, r % 4 : r % 4 + n, :])
 
         def load_grad(r, n=1):
-            nc.sync.dma_start(out=grad_row(r, n), in_=grad_v[r // 4, :, r % 4 : r % 4 + n, :])
+            g, j = divmod(r, 4)
+            nc.sync.dma_start(out=dmat[g][:, j : j + n, :], in_=grad_v[g, :, j : j + n, :])
 
         def load_x(k):
             nc.sync.dma_start(out=x_piece(k), in_=x_v[k])
@@ -102,13 +100,10 @@ def tile_blueboxlayer_pb_v_kernel(tc, Z, X, U, V, l1, mat, grad_out, out_0, out_
             bits = mat_rows(r)[:, 0, cols].bitcast(I32)
             nc.vector.tensor_single_scalar(out=bits, in_=bits, scalar=NO_SIGN, op=ALU.bitwise_and)
 
-        def mask(r):
-            for u in range(2):
-                pairs = "p (s q u e) -> p u s q e"
-                nc.vector.scalar_tensor_tensor(
-                    out=dmat[r // 4][:, r % 4, :].rearrange("p (s u q e) -> p u s q e", s=TG, u=2, e=2)[:, u],
-                    in0=mat_rows(r)[:, 0, :].rearrange(pairs, s=TG, u=2, e=2)[:, u], scalar=thres[:, 0:1],
-                    in1=grad_row(r)[:, 0, :].rearrange(pairs, s=TG, u=2, e=2)[:, u], op0=ALU.is_gt, op1=ALU.mult)
+        def mask(r, cols=slice(0, T)):
+            row = dmat[r // 4][:, r % 4, cols]
+            nc.vector.scalar_tensor_tensor(out=row, in0=mat_rows(r)[:, 0, cols], scalar=thres[:, 0:1], in1=row,
+                                           op0=ALU.is_gt, op1=ALU.mult)
 
         def transpose_x(k):
             words = x_piece(k).rearrange("p i t -> p (i t)").bitcast(F32)
@@ -143,8 +138,8 @@ def tile_blueboxlayer_pb_v_kernel(tc, Z, X, U, V, l1, mat, grad_out, out_0, out_
                     row, s = divmod(a, TG)
                     words = dmat[row // 4][:, row % 4, :].bitcast(F32)
                     for u in range(2):
-                        first = (2 * s + u) * P
-                        nc.tensor.transpose(bank[:, place, u, :], words[:, first : first + P], ident[:])
+                        first = (K // 2) * s + u
+                        nc.tensor.transpose(bank[:, place, u, :], words[:, first : first + K // 2 - 1 : 2], ident[:])
                 banks["row", part[0]] = bank
 
         def copy_rows(r, n=1, copy=scalar_copy, which=slice(None)):
@@ -211,8 +206,7 @@ def tile_blueboxlayer_pb_v_kernel(tc, Z, X, U, V, l1, mat, grad_out, out_0, out_
                     out=bank[:], lhsT=v_codes[k][:, g, cols].bitcast(E4M3), lhsT_scale=v_scales[k][:, g, cols],
                     rhs=d_codes[s][:, g, :].bitcast(E5M2), rhs_scale=d_scales[s][:, g, :],
                     start=(g == 0), stop=(g == DG - 1))
-            copy(out=stage[:, i, s * N : s * N + N].rearrange("p (q u e) -> p q u e", u=2, e=2),
-                 in_=bank[:].rearrange("p (u q e) -> p q u e", u=2, e=2))
+            copy(out=stage[:, i, s * N : s * N + N], in_=bank[:])
 
         def store_0(k, halves):
             nc.sync.dma_start(out=out_0v[k, :, halves, :], in_=big_tiles["out_0_", k][:, halves, :])

@@ -301,13 +301,12 @@ def tile_blueboxlayer_pb_v_kernel(tc, Z, X, U, V, l1, mat, grad_out, out_0, out_
         mask(6)
         copy_1(2, 1)
         product_1(0, 2)
-        store_1(0)
         multiply_1(1, 2)
         multiply_1(2, 2)
         multiply_1(3, 0)
         transpose_rows(4, 2)
         copy_1(1, 2)
-        store_1(1)
+        store_1(0, 2)
         copy_rows(4, 2)
         absolute_on_vector(7)
         quantize_rows(4, 2)
@@ -316,14 +315,12 @@ def tile_blueboxlayer_pb_v_kernel(tc, Z, X, U, V, l1, mat, grad_out, out_0, out_
         interleave_d(0, 2)
         quantize_d(0, 1)
         copy_1(2, 2)
-        store_1(2)
         copy_1(3, 0)
         product_1(3, 1)
         product_1(3, 2)
-        store_1(3)
+        store_1(2, 2)
         for c in range(MC):
             product_1(4, c)
-        store_1(4)
         quantize_d(0, 2)
         multiply_1(5, 0)
         transpose_rows(6, 2)
@@ -336,7 +333,7 @@ def tile_blueboxlayer_pb_v_kernel(tc, Z, X, U, V, l1, mat, grad_out, out_0, out_
         quantize_d(1, 0)
         product_1(5, 1)
         product_1(5, 2)
-        store_1(5)
+        store_1(4, 2)
         interleave_v(0, 0, scalar_copy)
         quantize_d(1, 1)
         for c in range(MC):

@@ -29,7 +29,7 @@ NO_SIGN = 0x7FFFFFFF
 
 BIG_SLOTS = 10
 TURNED_BUFS = 6
-GROUPED_BUFS = 3
+GROUPED_BUFS = 2
 
 
 def tile_blueboxlayer_pb_v_kernel(tc, Z, X, U, V, l1, mat, grad_out, out_0, out_1):
@@ -158,12 +158,12 @@ def tile_blueboxlayer_pb_v_kernel(tc, Z, X, U, V, l1, mat, grad_out, out_0, out_
 
         def interleave_d(g, s, part=slice(0, N), copy=vector_copy):
             if ("d", g, s) not in grouped:
-                grouped["d", g, s] = work.tile([P, N, 4], BF16, name="d_grouped", tag="grouped", align_bytes=64)
+                grouped["d", g, s] = work.tile([P, N, 4], BF16, name="d_grouped", align_bytes=64)
             copy(out=grouped["d", g, s][:, part].rearrange("p (c i) j -> p c j i", i=4),
                  in_=dmat[g][:, :, s * N : s * N + N][:, :, part].rearrange("p j (c i) -> p c j i", i=4))
 
         def interleave_v(g, k, copy=vector_copy):
-            grouped["v", g, k] = work.tile([P, 2 * P, 4], BF16, name="v_grouped", tag="grouped", align_bytes=64)
+            grouped["v", g, k] = work.tile([P, 2 * P, 4], BF16, name="v_grouped", align_bytes=64)
             copy(out=grouped["v", g, k][:].rearrange("p (i c h) j -> p c j i h", i=2, h=2),
                  in_=big_tiles["v", g][:, :, 2 * P * k : 2 * P * (k + 1)].rearrange("p j (c h i) -> p c j i h", h=2, i=2))
 
@@ -175,15 +175,16 @@ def tile_blueboxlayer_pb_v_kernel(tc, Z, X, U, V, l1, mat, grad_out, out_0, out_
             nc.vector.quantize_mx(out=v_codes[k][:, g, :].bitcast(E4M3), scales=v_scales[k][:, g, :],
                                   in_=grouped["v", g, k][:].rearrange("p n j -> p (n j)"))
 
-        def multiply_1(r, c):
-            bank = psum.tile([P, N], F32, name="bank_1", tag="bank")
-            for s in range(TG):
+        def multiply_1(r, c, passes=range(TG)):
+            if ("out_1", r, c) not in banks:
+                banks["out_1", r, c] = psum.tile([P, N], F32, name="bank_1", tag="bank")
+            bank = banks["out_1", r, c]
+            for s in passes:
                 cols = slice((TG * r + s) * P, (TG * r + s + 1) * P)
                 nc.tensor.matmul_mx(
                     out=bank[:], lhsT=dt_codes[:, cols].bitcast(E5M2), lhsT_scale=dt_scales[:, cols],
                     rhs=x_codes[c][:, s, :].bitcast(E4M3), rhs_scale=x_scales[c][:, s, :],
                     start=(s == 0), stop=(s == TG - 1))
-            banks["out_1", r, c] = bank
 
         def copy_1(r, c, copy=scalar_copy):
             stage = big_tile("out_1_", r // 2, [P, 2, M], F32)
@@ -193,9 +194,9 @@ def tile_blueboxlayer_pb_v_kernel(tc, Z, X, U, V, l1, mat, grad_out, out_0, out_
             multiply_1(r, c)
             copy_1(r, c, copy)
 
-        def store_1(r, n=1):
-            nc.sync.dma_start(out=out_1v[r // 4, :, r % 4 : r % 4 + n, :],
-                              in_=big_tiles["out_1_", r // 2][:, r % 2 : r % 2 + n, :])
+        def store_1(r, n=1, cols=slice(0, M)):
+            nc.sync.dma_start(out=out_1v[r // 4, :, r % 4 : r % 4 + n, cols],
+                              in_=big_tiles["out_1_", r // 2][:, r % 2 : r % 2 + n, cols])
 
         def product_0(k, i, s, copy):
             stage = big_tile("out_0_", k, [P, 2, T], F32)
@@ -227,13 +228,13 @@ def tile_blueboxlayer_pb_v_kernel(tc, Z, X, U, V, l1, mat, grad_out, out_0, out_
         load_grad(3, 1)
         load_x(4)
         load_x(5)
-        big_tile("out_1_", 0, [P, 2, M], F32)
-        load_mat(4, 1)
+        load_mat(4, 2)
         load_grad(4, 2)
-        load_mat(5, 1)
-        load_mat(6, 1)
+        load_mat(6, 2)
         load_grad(6, 2)
-        load_mat(7, 1)
+        big_tile("out_1_", 0, [P, 2, M], F32)
+        load_v(0)
+        load_v(1)
 
         vector_copy(out=l1_column[0:1, :], in_=l1_raw[:])
         bank_l1 = psum.tile([P, P], F32, name="bank_l1", tag="bank")
@@ -267,86 +268,81 @@ def tile_blueboxlayer_pb_v_kernel(tc, Z, X, U, V, l1, mat, grad_out, out_0, out_
         multiply_1(0, 0)
         multiply_1(0, 1)
         absolute(3)
+        mask(3)
+        multiply_1(1, 0)
+        transpose_rows(2)
+        multiply_1(1, 1)
         copy_1(0, 0)
         copy_1(0, 1)
-        mask(3)
-        load_v(0)
-        load_v(1)
-        product_1(1, 0)
-        transpose_rows(2)
-        transpose_x(4)
-        multiply_1(1, 1)
         copy_rows(2)
+        copy_1(1, 0)
+        transpose_x(4)
         copy_x(4)
-        interleave_d(0, 0)
         quantize_rows(2)
-        transpose_x(5)
-        transpose_rows(3)
-        absolute_on_vector(4)
-        quantize_x(4)
-        copy_x(5)
-        copy_rows(3)
-        quantize_x(5)
-        mask(4)
-        quantize_rows(3)
-        quantize_d(0, 0)
-        copy_1(1, 1)
+        interleave_d(0, 0)
         multiply_1(2, 0)
-        multiply_1(2, 1)
-        absolute(5)
-        mask(5)
+        transpose_x(5)
+        copy_1(1, 1)
         copy_1(2, 0)
-        absolute(6)
+        quantize_x(4, [0])
         interleave_d(0, 1, slice(0, N // 2))
-        mask(6)
+        quantize_x(4, [1, 2])
+        quantize_d(0, 0)
+        absolute_on_vector(4)
+        copy_x(5)
+        quantize_x(5)
+        multiply_1(2, 1)
+        transpose_rows(3)
+        absolute(5)
+        mask(4)
+        mask(5)
+        copy_rows(3)
+        absolute_on_vector(7)
+        quantize_rows(3)
+        mask(7)
         copy_1(2, 1)
         product_1(0, 2)
         multiply_1(1, 2)
         multiply_1(2, 2)
-        multiply_1(3, 0)
         transpose_rows(4, 2)
+        absolute(6)
+        copy_rows(4, 2)
+        quantize_rows(4, 2, slice(0, 2))
+        mask(6)
+        quantize_rows(4, 2, slice(2, 3))
         copy_1(1, 2)
         store_1(0, 2)
-        copy_rows(4, 2)
-        absolute_on_vector(7)
-        quantize_rows(4, 2)
-        mask(7)
-        interleave_d(0, 1, slice(N // 2, N))
-        interleave_d(0, 2)
-        quantize_d(0, 1)
         copy_1(2, 2)
-        copy_1(3, 0)
-        product_1(3, 1)
-        product_1(3, 2)
+        for c in range(MC):
+            product_1(3, c)
         store_1(2, 2)
+        interleave_d(0, 1, slice(N // 2, N))
+        interleave_d(1, 0)
+        quantize_d(0, 1)
         for c in range(MC):
             product_1(4, c)
-        quantize_d(0, 2)
-        multiply_1(5, 0)
         transpose_rows(6, 2)
         copy_rows(6, 2)
-        copy_1(5, 0)
-        interleave_d(1, 0, slice(0, N // 2))
-        quantize_rows(6, 2)
-        interleave_d(1, 0, slice(N // 2, N))
-        interleave_d(1, 1)
-        quantize_d(1, 0)
-        product_1(5, 1)
-        product_1(5, 2)
-        store_1(4, 2)
         interleave_v(0, 0, scalar_copy)
-        quantize_d(1, 1)
+        interleave_d(0, 2, slice(0, N // 2))
+        quantize_rows(6, 2)
+        quantize_d(1, 0)
+        interleave_d(0, 2, slice(N // 2, N))
+        interleave_d(1, 1)
+        quantize_d(0, 2)
         for c in range(MC):
-            product_1(6, c)
-        store_1(6)
-        quantize_v(0, 0)
+            product_1(5, c)
+        store_1(4, 2)
         interleave_v(1, 0, scalar_copy)
+        quantize_v(0, 0)
+        quantize_d(1, 1)
         interleave_d(1, 2)
         quantize_v(1, 0)
         quantize_d(1, 2)
-        for c in range(MC):
-            product_1(7, c)
-        store_1(7)
+        for r in range(6, ROWS):
+            for c in range(MC):
+                product_1(r, c)
+            store_1(r)
         for k in range(PIECES):
             more = k + 1 < PIECES
             if more:
@@ -354,13 +350,7 @@ def tile_blueboxlayer_pb_v_kernel(tc, Z, X, U, V, l1, mat, grad_out, out_0, out_
                 interleave_v(1, k + 1)
                 quantize_v(0, k + 1)
                 quantize_v(1, k + 1)
-            if k == 0:
-                for i, s in ((0, 0), (1, 0), (0, 1), (0, 2), (1, 1), (1, 2)):
-                    product_0(k, i, s, scalar_copy)
-                    if s == TG - 1:
-                        store_0(k, slice(i, i + 1))
-                continue
             for i in range(2):
                 for s in range(TG):
-                    product_0(k, i, s, vector_copy if (i == 1 and s != 1) or (not more and s == 1) else scalar_copy)
+                    product_0(k, i, s, scalar_copy if (more and i == 0) or (i + s) % 2 == 0 else vector_copy)
                 store_0(k, slice(i, i + 1))

@@ -53,7 +53,7 @@ def tile_blueboxlayer_pb_v_kernel(tc, Z, X, U, V, l1, mat, grad_out, out_0, out_
         grad_v = grad_out.rearrange("(g p j) t -> g p j t", g=DG, j=4)
         v_v = V.rearrange("(g p j) m -> g p j m", g=DG, j=4)
         x_v = X.rearrange("(k p i) t -> k p i t", p=P, i=2)
-        out_1v = out_1.rearrange("(g p j) m -> g p j m", g=DG, j=4)
+        out_1v = out_1.rearrange("(g p j) m -> g p (j m)", g=DG, j=4)
         out_0v = out_0.rearrange("(k p i) t -> k p i t", p=P, i=2)
 
         dmat = [keep.tile([P, 4, T], BF16, name="dmat%d" % g, align_bytes=256) for g in range(DG)]
@@ -194,9 +194,10 @@ def tile_blueboxlayer_pb_v_kernel(tc, Z, X, U, V, l1, mat, grad_out, out_0, out_
             multiply_1(r, c)
             copy_1(r, c, copy)
 
-        def store_1(r, n=1, cols=slice(0, M)):
-            nc.sync.dma_start(out=out_1v[r // 4, :, r % 4 : r % 4 + n, cols],
-                              in_=big_tiles["out_1_", r // 2][:, r % 2 : r % 2 + n, cols])
+        def store_1(r, c, n):
+            stage = big_tiles["out_1_", r // 2][:].rearrange("p j m -> p (j m)")
+            nc.sync.dma_start(out=out_1v[r // 4, :, (r % 4 * MC + c) * N : (r % 4 * MC + c + n) * N],
+                              in_=stage[:, (r % 2 * MC + c) * N : (r % 2 * MC + c + n) * N])
 
         def product_0(k, i, s, copy):
             stage = big_tile("out_0_", k, [P, 2, T], F32)
@@ -290,7 +291,9 @@ def tile_blueboxlayer_pb_v_kernel(tc, Z, X, U, V, l1, mat, grad_out, out_0, out_
         quantize_d(0, 0)
         absolute_on_vector(4)
         copy_x(5)
-        quantize_x(5)
+        quantize_x(5, [0])
+        interleave_d(0, 1, slice(N // 2, 3 * N // 4))
+        quantize_x(5, [1, 2])
         multiply_1(2, 1)
         transpose_rows(3)
         absolute(5)
@@ -299,6 +302,7 @@ def tile_blueboxlayer_pb_v_kernel(tc, Z, X, U, V, l1, mat, grad_out, out_0, out_
         copy_rows(3)
         absolute_on_vector(7)
         quantize_rows(3)
+        interleave_d(0, 1, slice(3 * N // 4, N))
         mask(7)
         copy_1(2, 1)
         product_1(0, 2)
@@ -311,38 +315,36 @@ def tile_blueboxlayer_pb_v_kernel(tc, Z, X, U, V, l1, mat, grad_out, out_0, out_
         mask(6)
         quantize_rows(4, 2, slice(2, 3))
         copy_1(1, 2)
-        store_1(0, 2)
+        store_1(0, 0, 2 * MC)
         copy_1(2, 2)
         for c in range(MC):
             product_1(3, c)
-        store_1(2, 2)
-        interleave_d(0, 1, slice(N // 2, N))
-        interleave_d(1, 0)
+        store_1(2, 0, 2 * MC)
+        interleave_d(0, 2)
         quantize_d(0, 1)
+        interleave_d(1, 0)
+        quantize_d(0, 2)
         for c in range(MC):
             product_1(4, c)
         transpose_rows(6, 2)
         copy_rows(6, 2)
         interleave_v(0, 0, scalar_copy)
-        interleave_d(0, 2, slice(0, N // 2))
-        quantize_rows(6, 2)
         quantize_d(1, 0)
-        interleave_d(0, 2, slice(N // 2, N))
+        quantize_rows(6, 2)
         interleave_d(1, 1)
-        quantize_d(0, 2)
+        interleave_d(1, 2)
         for c in range(MC):
             product_1(5, c)
-        store_1(4, 2)
+        store_1(4, 0, 2 * MC)
         interleave_v(1, 0, scalar_copy)
         quantize_v(0, 0)
-        quantize_d(1, 1)
-        interleave_d(1, 2)
         quantize_v(1, 0)
+        quantize_d(1, 1)
         quantize_d(1, 2)
-        for r in range(6, ROWS):
-            for c in range(MC):
-                product_1(r, c)
-            store_1(r)
+        for c in range(MC):
+            product_1(6, c)
+        product_1(7, 0)
+        store_1(6, 0, MC + 1)
         for k in range(PIECES):
             more = k + 1 < PIECES
             if more:
@@ -354,3 +356,6 @@ def tile_blueboxlayer_pb_v_kernel(tc, Z, X, U, V, l1, mat, grad_out, out_0, out_
                 for s in range(TG):
                     product_0(k, i, s, scalar_copy if (more and i == 0) or (i + s) % 2 == 0 else vector_copy)
                 store_0(k, slice(i, i + 1))
+        for c in range(1, MC):
+            product_1(7, c)
+            store_1(7, c, 1)

@@ -27,7 +27,7 @@ ROWS = 4 * DG
 PIECES = M // (2 * P)
 NO_SIGN = 0x7FFFFFFF
 
-BIG_SLOTS = 10
+BIG_SLOTS = 8
 TURNED_BUFS = 6
 GROUPED_BUFS = 2
 
@@ -51,12 +51,13 @@ def tile_blueboxlayer_pb_v_kernel(tc, Z, X, U, V, l1, mat, grad_out, out_0, out_
 
         mat_v = mat.rearrange("(g p j) t -> g p j t", g=DG, j=4)
         grad_v = grad_out.rearrange("(g p j) t -> g p j t", g=DG, j=4)
-        v_v = V.rearrange("(g p j) m -> g p j m", g=DG, j=4)
-        x_v = X.rearrange("(k p i) t -> k p i t", p=P, i=2)
+        v_v = V.rearrange("(g p j) m -> p g (j m)", g=DG, j=4)
+        x_v = X.rearrange("(k p i) t -> p k (i t)", p=P, i=2)
         out_1v = out_1.rearrange("(g p j) m -> g p (j m)", g=DG, j=4)
         out_0v = out_0.rearrange("(k p i) t -> k p i t", p=P, i=2)
 
         dmat = [keep.tile([P, 4, T], BF16, name="dmat%d" % g, align_bytes=256) for g in range(DG)]
+        v_rows = keep.tile([P, DG, 4, M], BF16, name="v_rows", align_bytes=256)
         dt_codes = keep.tile([P, ROWS * TG * P], U32, name="dt_codes", align_bytes=64)
         dt_scales = keep.tile([P, ROWS * TG * P], U8, name="dt_scales", align_bytes=64)
         x_codes = [keep.tile([P, TG, N], U32, name="x_codes%d" % c, align_bytes=64) for c in range(MC)]
@@ -76,8 +77,8 @@ def tile_blueboxlayer_pb_v_kernel(tc, Z, X, U, V, l1, mat, grad_out, out_0, out_
         def mat_rows(r, n=1):
             return big_tile("mat", r // 2, [P, 2, T], F32)[:, r % 2 : r % 2 + n, :]
 
-        def x_piece(k):
-            return big_tile("x", k // 2, [P, 2, 2, T], BF16)[:, k % 2]
+        def x_pieces(k, n=1):
+            return big_tile("x", k // 2, [P, 2, 2 * T], BF16)[:, k % 2 : k % 2 + n, :]
 
         def load_mat(r, n=1):
             nc.sync.dma_start(out=mat_rows(r, n), in_=mat_v[r // 4, :, r % 4 : r % 4 + n, :])
@@ -86,11 +87,11 @@ def tile_blueboxlayer_pb_v_kernel(tc, Z, X, U, V, l1, mat, grad_out, out_0, out_
             g, j = divmod(r, 4)
             nc.sync.dma_start(out=dmat[g][:, j : j + n, :], in_=grad_v[g, :, j : j + n, :])
 
-        def load_x(k):
-            nc.sync.dma_start(out=x_piece(k), in_=x_v[k])
+        def load_x(k, n=1):
+            nc.sync.dma_start(out=x_pieces(k, n), in_=x_v[:, k : k + n, :])
 
-        def load_v(g):
-            nc.sync.dma_start(out=big_tile("v", g, [P, 4, M], BF16)[:], in_=v_v[g])
+        def load_v():
+            nc.sync.dma_start(out=v_rows[:].rearrange("p g j m -> p g (j m)"), in_=v_v)
 
         def absolute(r, cols=slice(0, T)):
             row = mat_rows(r)[:, 0, cols]
@@ -106,7 +107,7 @@ def tile_blueboxlayer_pb_v_kernel(tc, Z, X, U, V, l1, mat, grad_out, out_0, out_
                                            op0=ALU.is_gt, op1=ALU.mult)
 
         def transpose_x(k):
-            words = x_piece(k).rearrange("p i t -> p (i t)").bitcast(F32)
+            words = x_pieces(k)[:, 0, :].bitcast(F32)
             for s in range(TG):
                 bank = psum.tile([P, 4, P], F32, name="bank_x", tag="bank")
                 for i in range(2):
@@ -165,7 +166,7 @@ def tile_blueboxlayer_pb_v_kernel(tc, Z, X, U, V, l1, mat, grad_out, out_0, out_
         def interleave_v(g, k, copy=vector_copy):
             grouped["v", g, k] = work.tile([P, 2 * P, 4], BF16, name="v_grouped", align_bytes=64)
             copy(out=grouped["v", g, k][:].rearrange("p (i c h) j -> p c j i h", i=2, h=2),
-                 in_=big_tiles["v", g][:, :, 2 * P * k : 2 * P * (k + 1)].rearrange("p j (c h i) -> p c j i h", h=2, i=2))
+                 in_=v_rows[:, g, :, 2 * P * k : 2 * P * (k + 1)].rearrange("p j (c h i) -> p c j i h", h=2, i=2))
 
         def quantize_d(g, s):
             nc.vector.quantize_mx(out=d_codes[s][:, g, :].bitcast(E5M2), scales=d_scales[s][:, g, :],
@@ -194,6 +195,17 @@ def tile_blueboxlayer_pb_v_kernel(tc, Z, X, U, V, l1, mat, grad_out, out_0, out_
             multiply_1(r, c)
             copy_1(r, c, copy)
 
+        def half_product_1(r, c, h, copy):
+            half = slice(h * N // 2, (h + 1) * N // 2)
+            bank = psum.tile([P, N // 2], F32, name="bank_half", tag="bank")
+            for s in range(TG):
+                cols = slice((TG * r + s) * P, (TG * r + s + 1) * P)
+                nc.tensor.matmul_mx(
+                    out=bank[:], lhsT=dt_codes[:, cols].bitcast(E5M2), lhsT_scale=dt_scales[:, cols],
+                    rhs=x_codes[c][:, s, half].bitcast(E4M3), rhs_scale=x_scales[c][:, s, half],
+                    start=(s == 0), stop=(s == TG - 1))
+            copy(out=big_tiles["out_1_", r // 2][:, r % 2, c * N : c * N + N][:, half], in_=bank[:])
+
         def store_1(r, c, n):
             stage = big_tiles["out_1_", r // 2][:].rearrange("p j m -> p (j m)")
             nc.sync.dma_start(out=out_1v[r // 4, :, (r % 4 * MC + c) * N : (r % 4 * MC + c + n) * N],
@@ -216,9 +228,8 @@ def tile_blueboxlayer_pb_v_kernel(tc, Z, X, U, V, l1, mat, grad_out, out_0, out_
         nc.scalar.dma_start(out=l1_raw[:], in_=l1.rearrange("(a b) -> a b", a=1))
         nc.vector.memset(l1_column[:], 0.0)
         load_mat(0, 1)
-        load_grad(0, 1)
+        load_grad(0, 2)
         load_mat(1, 1)
-        load_grad(1, 1)
         load_x(0)
         load_x(1)
         load_x(2)
@@ -233,9 +244,7 @@ def tile_blueboxlayer_pb_v_kernel(tc, Z, X, U, V, l1, mat, grad_out, out_0, out_
         load_grad(4, 2)
         load_mat(6, 2)
         load_grad(6, 2)
-        big_tile("out_1_", 0, [P, 2, M], F32)
-        load_v(0)
-        load_v(1)
+        load_v()
 
         vector_copy(out=l1_column[0:1, :], in_=l1_raw[:])
         bank_l1 = psum.tile([P, P], F32, name="bank_l1", tag="bank")
@@ -250,37 +259,41 @@ def tile_blueboxlayer_pb_v_kernel(tc, Z, X, U, V, l1, mat, grad_out, out_0, out_
         copy_rows(0)
         transpose_x(0)
         copy_x(0)
+        transpose_rows(1)
         quantize_rows(0)
         transpose_x(1)
-        quantize_x(0)
+        quantize_x(0, [0])
+        copy_rows(1, 1, vector_copy)
+        quantize_x(0, [1, 2])
+        quantize_rows(1)
         copy_x(1)
         transpose_x(2)
         quantize_x(1)
         copy_x(2)
         transpose_x(3)
-        transpose_rows(1)
-        quantize_x(2)
-        copy_x(3)
+        quantize_x(2, [0, 1])
         absolute_on_vector(2)
-        copy_rows(1)
+        quantize_x(2, [2])
+        copy_x(3)
         quantize_x(3)
-        quantize_rows(1)
-        mask(2)
+        mask(2, slice(0, 2 * K))
+        mask(2, slice(2 * K, T))
         multiply_1(0, 0)
-        multiply_1(0, 1)
-        absolute(3)
-        mask(3)
         multiply_1(1, 0)
+        multiply_1(0, 1)
+        copy_1(0, 0)
+        for half in (slice(0, T // 2), slice(T // 2, T)):
+            absolute(3, half)
+            mask(3, half)
         transpose_rows(2)
         multiply_1(1, 1)
-        copy_1(0, 0)
+        copy_1(1, 0)
         copy_1(0, 1)
         copy_rows(2)
-        copy_1(1, 0)
         transpose_x(4)
         copy_x(4)
-        quantize_rows(2)
         interleave_d(0, 0)
+        quantize_rows(2)
         multiply_1(2, 0)
         transpose_x(5)
         copy_1(1, 1)
@@ -288,40 +301,38 @@ def tile_blueboxlayer_pb_v_kernel(tc, Z, X, U, V, l1, mat, grad_out, out_0, out_
         quantize_x(4, [0])
         interleave_d(0, 1, slice(0, N // 2))
         quantize_x(4, [1, 2])
+        interleave_d(0, 1, slice(N // 2, N))
         quantize_d(0, 0)
         absolute_on_vector(4)
         copy_x(5)
-        quantize_x(5, [0])
-        interleave_d(0, 1, slice(N // 2, 3 * N // 4))
-        quantize_x(5, [1, 2])
+        quantize_x(5)
         multiply_1(2, 1)
         transpose_rows(3)
         absolute(5)
         mask(4)
         mask(5)
         copy_rows(3)
-        absolute_on_vector(7)
         quantize_rows(3)
-        interleave_d(0, 1, slice(3 * N // 4, N))
-        mask(7)
+        absolute_on_vector(7)
+        quantize_d(0, 1)
         copy_1(2, 1)
         product_1(0, 2)
         multiply_1(1, 2)
         multiply_1(2, 2)
         transpose_rows(4, 2)
-        absolute(6)
-        copy_rows(4, 2)
-        quantize_rows(4, 2, slice(0, 2))
-        mask(6)
-        quantize_rows(4, 2, slice(2, 3))
         copy_1(1, 2)
+        copy_rows(4, 2)
+        quantize_rows(4, 2, slice(0, 1))
+        mask(7)
+        absolute(6)
+        quantize_rows(4, 2, slice(1, 3))
+        mask(6)
         store_1(0, 0, 2 * MC)
         copy_1(2, 2)
         for c in range(MC):
             product_1(3, c)
         store_1(2, 0, 2 * MC)
         interleave_d(0, 2)
-        quantize_d(0, 1)
         interleave_d(1, 0)
         quantize_d(0, 2)
         for c in range(MC):
@@ -356,6 +367,7 @@ def tile_blueboxlayer_pb_v_kernel(tc, Z, X, U, V, l1, mat, grad_out, out_0, out_
                 for s in range(TG):
                     product_0(k, i, s, scalar_copy if (more and i == 0) or (i + s) % 2 == 0 else vector_copy)
                 store_0(k, slice(i, i + 1))
-        for c in range(1, MC):
-            product_1(7, c)
-            store_1(7, c, 1)
+        product_1(7, 1)
+        half_product_1(7, 2, 0, vector_copy)
+        half_product_1(7, 2, 1, scalar_copy)
+        store_1(7, 1, 2)

from contextlib import ExitStack

import concourse.mybir as mybir
from concourse.masks import make_identity

D, T, M = 1024, 1536, 1536
FLOPS = 2 * 2 * D * T * M
BYTES = 2 * (M * T + D * M + D * T) + 4 * (D * T + M * T + D * M) + 2

F32 = mybir.dt.float32
BF16 = mybir.dt.bfloat16
I32 = mybir.dt.int32
U32 = mybir.dt.uint32
U8 = mybir.dt.uint8
E4M3 = mybir.dt.float8_e4m3fn_x4
E5M2 = mybir.dt.float8_e5m2_x4
ALU = mybir.AluOpType
ABS = mybir.ActivationFunctionType.Abs

P = 128
K = 512
N = 512
DG = D // K
TG = T // K
MC = M // N
ROWS = 4 * DG
PIECES = M // (2 * P)
NO_SIGN = 0x7FFFFFFF

BIG_SLOTS = 8
TURNED_BUFS = 6
GROUPED_BUFS = 2


def tile_blueboxlayer_pb_v_kernel(tc, Z, X, U, V, l1, mat, grad_out, out_0, out_1):
    nc = tc.nc
    vector_copy, scalar_copy = nc.vector.tensor_copy, nc.scalar.copy
    with ExitStack() as ctx:
        const = ctx.enter_context(tc.tile_pool(name="const", bufs=1))
        big = ctx.enter_context(tc.tile_pool(name="big", bufs=BIG_SLOTS))
        keep = ctx.enter_context(tc.tile_pool(name="keep", bufs=1))
        work = ctx.enter_context(tc.tile_pool(name="work", bufs=GROUPED_BUFS))
        psum = ctx.enter_context(tc.psum_pool(name="psum", bufs=8))
        ctx.enter_context(tc.manual_schedule())

        thres = const.tile([P, 1], F32, name="thres")
        l1_raw = const.tile([1, 1], BF16, name="l1_raw")
        l1_column = const.tile([P, 1], F32, name="l1_column")
        ident = const.tile([P, P], F32, name="ident")
        make_identity(nc, ident[:])

        mat_v = mat.rearrange("(g p j) t -> g p j t", g=DG, j=4)
        grad_v = grad_out.rearrange("(g p j) t -> g p j t", g=DG, j=4)
        v_v = V.rearrange("(g p j) m -> p g (j m)", g=DG, j=4)
        x_v = X.rearrange("(k p i) t -> p k (i t)", p=P, i=2)
        out_1v = out_1.rearrange("(g p j) m -> g p (j m)", g=DG, j=4)
        out_0v = out_0.rearrange("(k p i) t -> k p i t", p=P, i=2)

        dmat = [keep.tile([P, 4, T], BF16, name="dmat%d" % g, align_bytes=256) for g in range(DG)]
        v_rows = keep.tile([P, DG, 4, M], BF16, name="v_rows", align_bytes=256)
        dt_codes = keep.tile([P, ROWS * TG * P], U32, name="dt_codes", align_bytes=64)
        dt_scales = keep.tile([P, ROWS * TG * P], U8, name="dt_scales", align_bytes=64)
        x_codes = [keep.tile([P, TG, N], U32, name="x_codes%d" % c, align_bytes=64) for c in range(MC)]
        x_scales = [keep.tile([P, TG, N], U8, name="x_scales%d" % c, align_bytes=64) for c in range(MC)]
        d_codes = [keep.tile([P, DG, N], U32, name="d_codes%d" % s, align_bytes=64) for s in range(TG)]
        d_scales = [keep.tile([P, DG, N], U8, name="d_scales%d" % s, align_bytes=64) for s in range(TG)]
        v_codes = [keep.tile([P, DG, 2 * P], U32, name="v_codes%d" % k, align_bytes=64) for k in range(PIECES)]
        v_scales = [keep.tile([P, DG, 2 * P], U8, name="v_scales%d" % k, align_bytes=64) for k in range(PIECES)]

        big_tiles, banks, turned, grouped = {}, {}, {}, {}

        def big_tile(kind, index, shape, dtype):
            if (kind, index) not in big_tiles:
                big_tiles[kind, index] = big.tile(shape, dtype, name="%s%d" % (kind, index), tag="big", align_bytes=256)
            return big_tiles[kind, index]

        def mat_rows(r, n=1):
            return big_tile("mat", r // 2, [P, 2, T], F32)[:, r % 2 : r % 2 + n, :]

        def x_pieces(k, n=1):
            return big_tile("x", k // 2, [P, 2, 2 * T], BF16)[:, k % 2 : k % 2 + n, :]

        def load_mat(r, n=1):
            nc.sync.dma_start(out=mat_rows(r, n), in_=mat_v[r // 4, :, r % 4 : r % 4 + n, :])

        def load_grad(r, n=1):
            g, j = divmod(r, 4)
            nc.sync.dma_start(out=dmat[g][:, j : j + n, :], in_=grad_v[g, :, j : j + n, :])

        def load_x(k, n=1):
            nc.sync.dma_start(out=x_pieces(k, n), in_=x_v[:, k : k + n, :])

        def load_v():
            nc.sync.dma_start(out=v_rows[:].rearrange("p g j m -> p g (j m)"), in_=v_v)

        def absolute(r, cols=slice(0, T)):
            row = mat_rows(r)[:, 0, cols]
            nc.scalar.activation(out=row, in_=row, func=ABS)

        def absolute_on_vector(r, cols=slice(0, T)):
            bits = mat_rows(r)[:, 0, cols].bitcast(I32)
            nc.vector.tensor_single_scalar(out=bits, in_=bits, scalar=NO_SIGN, op=ALU.bitwise_and)

        def mask(r, cols=slice(0, T)):
            row = dmat[r // 4][:, r % 4, cols]
            nc.vector.scalar_tensor_tensor(out=row, in0=mat_rows(r)[:, 0, cols], scalar=thres[:, 0:1], in1=row,
                                           op0=ALU.is_gt, op1=ALU.mult)

        def transpose_x(k):
            words = x_pieces(k)[:, 0, :].bitcast(F32)
            for s in range(TG):
                bank = psum.tile([P, 4, P], F32, name="bank_x", tag="bank")
                for i in range(2):
                    for u in range(2):
                        first = i * (T // 2) + (K // 2) * s + u
                        nc.tensor.transpose(bank[:, 2 * i + u, :], words[:, first : first + K // 2 - 1 : 2], ident[:])
                banks["x", k, s] = bank

        def copy_x(k, passes=range(TG), copy=scalar_copy):
            for s in passes:
                dest = work.tile([P, 2 * K], BF16, name="x_turned", tag="turned", bufs=TURNED_BUFS, align_bytes=64)
                copy(out=dest[:].bitcast(F32).rearrange("q (p w) -> q p w", w=4),
                     in_=banks["x", k, s][:].rearrange("q w p -> q p w"))
                turned["x", k, s] = dest

        def quantize_x(k, passes=range(TG)):
            half = slice((k % 2) * N // 2, (k % 2 + 1) * N // 2)
            for s in passes:
                nc.vector.quantize_mx(out=x_codes[k // 2][:, s, half].bitcast(E4M3),
                                      scales=x_scales[k // 2][:, s, half], in_=turned["x", k, s][:])

        def bank_parts(r, n):
            return [range(a, min(a + 2, TG * (r + n))) for a in range(TG * r, TG * (r + n), 2)]

        def transpose_rows(r, n=1):
            for part in bank_parts(r, n):
                bank = psum.tile([P, len(part), 2, P], F32, name="bank_row", tag="bank")
                for place, a in enumerate(part):
                    row, s = divmod(a, TG)
                    words = dmat[row // 4][:, row % 4, :].bitcast(F32)
                    for u in range(2):
                        first = (K // 2) * s + u
                        nc.tensor.transpose(bank[:, place, u, :], words[:, first : first + K // 2 - 1 : 2], ident[:])
                banks["row", part[0]] = bank

        def copy_rows(r, n=1, copy=scalar_copy, which=slice(None)):
            for part in bank_parts(r, n)[which]:
                dest = work.tile([P, len(part) * K], BF16, name="row_turned", tag="turned", bufs=TURNED_BUFS,
                                 align_bytes=64)
                copy(out=dest[:].bitcast(F32).rearrange("q (s p u) -> q s p u", s=len(part), u=2),
                     in_=banks["row", part[0]][:].rearrange("q s u p -> q s p u"))
                turned["row", part[0]] = dest

        def quantize_rows(r, n=1, which=slice(None)):
            for part in bank_parts(r, n)[which]:
                cols = slice(part[0] * P, (part[-1] + 1) * P)
                nc.vector.quantize_mx(out=dt_codes[:, cols].bitcast(E5M2), scales=dt_scales[:, cols],
                                      in_=turned["row", part[0]][:])

        def interleave_d(g, s, part=slice(0, N), copy=vector_copy):
            if ("d", g, s) not in grouped:
                grouped["d", g, s] = work.tile([P, N, 4], BF16, name="d_grouped", align_bytes=64)
            copy(out=grouped["d", g, s][:, part].rearrange("p (c i) j -> p c j i", i=4),
                 in_=dmat[g][:, :, s * N : s * N + N][:, :, part].rearrange("p j (c i) -> p c j i", i=4))

        def interleave_v(g, k, copy=vector_copy):
            grouped["v", g, k] = work.tile([P, 2 * P, 4], BF16, name="v_grouped", align_bytes=64)
            copy(out=grouped["v", g, k][:].rearrange("p (i c h) j -> p c j i h", i=2, h=2),
                 in_=v_rows[:, g, :, 2 * P * k : 2 * P * (k + 1)].rearrange("p j (c h i) -> p c j i h", h=2, i=2))

        def quantize_d(g, s):
            nc.vector.quantize_mx(out=d_codes[s][:, g, :].bitcast(E5M2), scales=d_scales[s][:, g, :],
                                  in_=grouped["d", g, s][:].rearrange("p n j -> p (n j)"))

        def quantize_v(g, k):
            nc.vector.quantize_mx(out=v_codes[k][:, g, :].bitcast(E4M3), scales=v_scales[k][:, g, :],
                                  in_=grouped["v", g, k][:].rearrange("p n j -> p (n j)"))

        def multiply_1(r, c, passes=range(TG)):
            if ("out_1", r, c) not in banks:
                banks["out_1", r, c] = psum.tile([P, N], F32, name="bank_1", tag="bank")
            bank = banks["out_1", r, c]
            for s in passes:
                cols = slice((TG * r + s) * P, (TG * r + s + 1) * P)
                nc.tensor.matmul_mx(
                    out=bank[:], lhsT=dt_codes[:, cols].bitcast(E5M2), lhsT_scale=dt_scales[:, cols],
                    rhs=x_codes[c][:, s, :].bitcast(E4M3), rhs_scale=x_scales[c][:, s, :],
                    start=(s == 0), stop=(s == TG - 1))

        def copy_1(r, c, copy=scalar_copy):
            stage = big_tile("out_1_", r // 2, [P, 2, M], F32)
            copy(out=stage[:, r % 2, c * N : c * N + N], in_=banks["out_1", r, c][:])

        def product_1(r, c, copy=scalar_copy):
            multiply_1(r, c)
            copy_1(r, c, copy)

        def half_product_1(r, c, h, copy):
            half = slice(h * N // 2, (h + 1) * N // 2)
            bank = psum.tile([P, N // 2], F32, name="bank_half", tag="bank")
            for s in range(TG):
                cols = slice((TG * r + s) * P, (TG * r + s + 1) * P)
                nc.tensor.matmul_mx(
                    out=bank[:], lhsT=dt_codes[:, cols].bitcast(E5M2), lhsT_scale=dt_scales[:, cols],
                    rhs=x_codes[c][:, s, half].bitcast(E4M3), rhs_scale=x_scales[c][:, s, half],
                    start=(s == 0), stop=(s == TG - 1))
            copy(out=big_tiles["out_1_", r // 2][:, r % 2, c * N : c * N + N][:, half], in_=bank[:])

        def store_1(r, c, n):
            stage = big_tiles["out_1_", r // 2][:].rearrange("p j m -> p (j m)")
            nc.sync.dma_start(out=out_1v[r // 4, :, (r % 4 * MC + c) * N : (r % 4 * MC + c + n) * N],
                              in_=stage[:, (r % 2 * MC + c) * N : (r % 2 * MC + c + n) * N])

        def product_0(k, i, s, copy):
            stage = big_tile("out_0_", k, [P, 2, T], F32)
            cols = slice(i * P, i * P + P)
            bank = psum.tile([P, N], F32, name="bank_0", tag="bank")
            for g in range(DG):
                nc.tensor.matmul_mx(
                    out=bank[:], lhsT=v_codes[k][:, g, cols].bitcast(E4M3), lhsT_scale=v_scales[k][:, g, cols],
                    rhs=d_codes[s][:, g, :].bitcast(E5M2), rhs_scale=d_scales[s][:, g, :],
                    start=(g == 0), stop=(g == DG - 1))
            copy(out=stage[:, i, s * N : s * N + N], in_=bank[:])

        def store_0(k, halves):
            nc.sync.dma_start(out=out_0v[k, :, halves, :], in_=big_tiles["out_0_", k][:, halves, :])

        nc.scalar.dma_start(out=l1_raw[:], in_=l1.rearrange("(a b) -> a b", a=1))
        nc.vector.memset(l1_column[:], 0.0)
        load_mat(0, 1)
        load_grad(0, 2)
        load_mat(1, 1)
        load_x(0)
        load_x(1)
        load_x(2)
        load_x(3)
        load_mat(2, 1)
        load_grad(2, 1)
        load_mat(3, 1)
        load_grad(3, 1)
        load_x(4)
        load_x(5)
        load_mat(4, 2)
        load_grad(4, 2)
        load_mat(6, 2)
        load_grad(6, 2)
        load_v()

        vector_copy(out=l1_column[0:1, :], in_=l1_raw[:])
        bank_l1 = psum.tile([P, P], F32, name="bank_l1", tag="bank")
        nc.tensor.transpose(bank_l1[:], l1_column[:].to_broadcast([P, P]), ident[:])
        vector_copy(out=thres[:], in_=bank_l1[:, 0:1])

        absolute_on_vector(0)
        mask(0)
        absolute_on_vector(1)
        transpose_rows(0)
        mask(1)
        copy_rows(0)
        transpose_x(0)
        copy_x(0)
        transpose_rows(1)
        quantize_rows(0)
        transpose_x(1)
        quantize_x(0, [0])
        copy_rows(1, 1, vector_copy)
        quantize_x(0, [1, 2])
        quantize_rows(1)
        copy_x(1)
        transpose_x(2)
        quantize_x(1)
        copy_x(2)
        transpose_x(3)
        quantize_x(2, [0, 1])
        absolute_on_vector(2)
        quantize_x(2, [2])
        copy_x(3)
        quantize_x(3)
        mask(2, slice(0, 2 * K))
        mask(2, slice(2 * K, T))
        multiply_1(0, 0)
        multiply_1(1, 0)
        multiply_1(0, 1)
        copy_1(0, 0)
        for half in (slice(0, T // 2), slice(T // 2, T)):
            absolute(3, half)
            mask(3, half)
        transpose_rows(2)
        multiply_1(1, 1)
        copy_1(1, 0)
        copy_1(0, 1)
        copy_rows(2)
        transpose_x(4)
        copy_x(4)
        interleave_d(0, 0)
        quantize_rows(2)
        multiply_1(2, 0)
        transpose_x(5)
        copy_1(1, 1)
        copy_1(2, 0)
        quantize_x(4, [0])
        interleave_d(0, 1, slice(0, N // 2))
        quantize_x(4, [1, 2])
        interleave_d(0, 1, slice(N // 2, N))
        quantize_d(0, 0)
        absolute_on_vector(4)
        copy_x(5)
        quantize_x(5)
        multiply_1(2, 1)
        transpose_rows(3)
        absolute(5)
        mask(4)
        mask(5)
        copy_rows(3)
        quantize_rows(3)
        absolute_on_vector(7)
        quantize_d(0, 1)
        copy_1(2, 1)
        product_1(0, 2)
        multiply_1(1, 2)
        multiply_1(2, 2)
        transpose_rows(4, 2)
        copy_1(1, 2)
        copy_rows(4, 2)
        quantize_rows(4, 2, slice(0, 1))
        mask(7)
        absolute(6)
        quantize_rows(4, 2, slice(1, 3))
        mask(6)
        store_1(0, 0, 2 * MC)
        copy_1(2, 2)
        for c in range(MC):
            product_1(3, c)
        store_1(2, 0, 2 * MC)
        interleave_d(0, 2)
        interleave_d(1, 0)
        quantize_d(0, 2)
        for c in range(MC):
            product_1(4, c)
        transpose_rows(6, 2)
        copy_rows(6, 2)
        interleave_v(0, 0, scalar_copy)
        quantize_d(1, 0)
        quantize_rows(6, 2)
        interleave_d(1, 1)
        interleave_d(1, 2)
        for c in range(MC):
            product_1(5, c)
        store_1(4, 0, 2 * MC)
        interleave_v(1, 0, scalar_copy)
        quantize_v(0, 0)
        quantize_v(1, 0)
        quantize_d(1, 1)
        quantize_d(1, 2)
        for c in range(MC):
            product_1(6, c)
        product_1(7, 0)
        store_1(6, 0, MC + 1)
        for k in range(PIECES):
            more = k + 1 < PIECES
            if more:
                interleave_v(0, k + 1)
                interleave_v(1, k + 1)
                quantize_v(0, k + 1)
                quantize_v(1, k + 1)
            for i in range(2):
                for s in range(TG):
                    product_0(k, i, s, scalar_copy if (more and i == 0) or (i + s) % 2 == 0 else vector_copy)
                store_0(k, slice(i, i + 1))
        product_1(7, 1)
        half_product_1(7, 2, 0, vector_copy)
        half_product_1(7, 2, 1, scalar_copy)
        store_1(7, 1, 2)
